import numpy as np
import ml_dtypes


def mxq(x, axis, fmt="e4m3"):
    dtype, down = {"e4m3": (ml_dtypes.float8_e4m3fn, 7), "e5m2": (ml_dtypes.float8_e5m2, 14)}[fmt]
    v = np.moveaxis(np.asarray(x, np.float32).astype(ml_dtypes.bfloat16).astype(np.float64), axis, -1)
    blocks = v.reshape(v.shape[:-1] + (-1, 32))
    amax = np.abs(blocks).max(-1, keepdims=True)
    byte = np.maximum(np.where(amax > 0, np.frexp(amax)[1] - 1 + 127, 0) - down, 1)
    scale = np.exp2(byte - 127.0)
    codes = (blocks / scale).astype(np.float32).astype(dtype).astype(np.float64)
    return np.moveaxis((codes * scale).reshape(v.shape), -1, axis)


WIDE = False


def mx_kscale(k):
    if not WIDE:
        return np.ones(k)
    levels = np.array([10, -10, 5, -5, 0])
    a = np.random.permutation(np.resize(levels, k // 512 * 4)).reshape(k // 512, 4)
    idx = np.arange(k)
    return np.exp2(a[idx // 512, idx % 128 // 32])


BF16 = ml_dtypes.bfloat16


def bf(x):
    return np.asarray(x, np.float32).astype(BF16)


def f64(x):
    return np.asarray(x).astype(np.float64)


B, E, M, NH, NKV, HD, D = 2, 256, 1024, 16, 8, 128, 2048
G = NH // NKV
A = NH * HD
SCALE = 0.5
QK = 2.0 / HD ** 0.25


def setup_inputs():
    t = mx_kscale(A).reshape(NKV, G, HD)[:, 0, :]
    tq = np.repeat(t, G, axis=0).reshape(A)
    sgn = np.where(np.random.standard_normal((NKV, HD)) > 0.0, 1.0, -1.0)
    v = sgn * (2.0 + 1.5 * np.random.uniform(-1.0, 1.0, (B, M, NKV, HD)))
    return {"q_pos": bf(np.random.standard_normal((E, NH, HD)) * QK),
            "k_mem": bf(np.random.standard_normal((B, M, NKV, HD)) * QK),
            "v_mem": bf(v * t),
            "Wo": bf(np.random.standard_normal((D, A)) / np.sqrt(A) / tq)}


def reference(q_pos, k_mem, v_mem, Wo):
    q = f64(q_pos).transpose(1, 0, 2).reshape(NKV, G * E, HD)
    kt = f64(k_mem).transpose(0, 2, 3, 1)
    v = f64(v_mem).transpose(0, 2, 1, 3)
    s = (q @ kt) * SCALE
    e = np.exp(s - s.max(-1, keepdims=True))
    o = (mxq(e, 3, "e4m3") @ mxq(v, 2, "e4m3")) / e.sum(-1, keepdims=True)
    a = o.reshape(B, NKV, G, E, HD).transpose(0, 3, 1, 2, 4).reshape(B, E, A)
    return mxq(a, 2, "e4m3") @ mxq(f64(Wo).T, 0, "e4m3")

@@ -1,0 +1,262 @@
+from contextlib import ExitStack
+
+import concourse.masks as masks
+import concourse.mybir as mybir
+
+BF16 = mybir.dt.bfloat16
+F32 = mybir.dt.float32
+U32 = mybir.dt.uint32
+U8 = mybir.dt.uint8
+FP8X4 = mybir.dt.float8_e4m3fn_x4
+EXP = mybir.ActivationFunctionType.Exp
+ALU = mybir.AluOpType
+ALONG_ROW = mybir.AxisListType.X
+
+P = 128
+PACK = 4
+K_PASS = P * PACK
+
+BATCH = 2
+QUERIES = 256
+SLOTS = 1024
+HEADS = 16
+KV_HEADS = 8
+GROUP = HEADS // KV_HEADS
+HEAD_DIM = 128
+FEATURES = HEADS * HEAD_DIM
+MODEL = 2048
+SCORE_FACTOR = 0.5
+
+QUERY_TILES = QUERIES // P
+SLOT_PASSES = SLOTS // K_PASS
+FEATURE_PASSES = FEATURES // K_PASS
+BLOCKS = 2 * PACK
+OUT_COLS = 512
+OUT_BLOCKS = MODEL // OUT_COLS
+WO_ROWS = 2 * P
+
+FLOPS = 2 * (2 * BATCH * HEADS * QUERIES * SLOTS * HEAD_DIM) + 2 * BATCH * QUERIES * FEATURES * MODEL
+
+
+def tile_qwen2dymemdecoderlayer_pa_kernel(tc, q_pos, k_mem, v_mem, Wo, out):
+    nc = tc.nc
+    with ExitStack() as ctx:
+        keep = ctx.enter_context(tc.tile_pool(name="keep", bufs=1))
+        loads = ctx.enter_context(tc.tile_pool(name="loads", bufs=3))
+        work = ctx.enter_context(tc.tile_pool(name="work", bufs=3))
+        codes_pool = ctx.enter_context(tc.tile_pool(name="codes", bufs=6))
+        small = ctx.enter_context(tc.tile_pool(name="small", bufs=6))
+        psum_scores = ctx.enter_context(tc.psum_pool(name="psum_scores", bufs=4))
+        psum_et = ctx.enter_context(tc.psum_pool(name="psum_et", bufs=1))
+        psum_o = ctx.enter_context(tc.psum_pool(name="psum_o", bufs=1))
+        psum_misc = ctx.enter_context(tc.psum_pool(name="psum_misc", bufs=2))
+
+        ident_bf16 = keep.tile([P, P], BF16)
+        masks.make_identity(nc, ident_bf16[:])
+        ident_f32 = keep.tile([P, P], F32)
+        masks.make_identity(nc, ident_f32[:])
+
+        q_t = keep.tile([P, QUERY_TILES, HEADS, P], BF16)
+        k_t = keep.tile([P, BATCH * KV_HEADS, SLOTS], BF16)
+        v_codes = keep.tile([P, BATCH * KV_HEADS, SLOT_PASSES * HEAD_DIM], U32, align_bytes=64)
+        v_scales = keep.tile([P, BATCH * KV_HEADS, SLOT_PASSES * HEAD_DIM], U8, align_bytes=64)
+        wo_codes = keep.tile([P, FEATURE_PASSES, MODEL], U32, align_bytes=64)
+        wo_scales = keep.tile([P, FEATURE_PASSES, MODEL], U8, align_bytes=64)
+        a_codes = keep.tile([P, BATCH * QUERY_TILES, FEATURE_PASSES * P], U32, align_bytes=64)
+        a_scales = keep.tile([P, BATCH * QUERY_TILES, FEATURE_PASSES * P], U8, align_bytes=64)
+
+        def quantise(codes, scales, grouped):
+            nc.vector.quantize_mx(out=codes.bitcast(FP8X4), scales=scales, in_=grouped)
+
+        def transpose_blocks(bank, rows):
+            for x in range(BLOCKS):
+                nc.tensor.transpose(out=bank[:, x, :], in_=rows[:, x * P : (x + 1) * P], identity=ident_bf16[:])
+
+        def group_words(copy, bank):
+            grouped = work.tile([P, 2, P, PACK], BF16, tag="grouped", align_bytes=64)
+            copy(out=grouped[:], in_=bank[:].rearrange("p (c t) r -> p c r t", t=PACK))
+            return grouped[:].rearrange("p c r t -> p (c r t)")
+
+        def prepare_queries(query_tile):
+            q_rows = loads.tile([P, HEADS * HEAD_DIM], BF16, tag="q_rows")
+            nc.sync.dma_start(
+                out=q_rows[:], in_=q_pos[query_tile * P : (query_tile + 1) * P].rearrange("q h d -> q (h d)")
+            )
+            for half in range(HEADS // BLOCKS):
+                bank = psum_misc.tile([P, BLOCKS, P], BF16, tag="misc")
+                transpose_blocks(bank, q_rows[:, half * BLOCKS * P : (half + 1) * BLOCKS * P])
+                nc.vector.tensor_copy(out=q_t[:, query_tile, half * BLOCKS : (half + 1) * BLOCKS, :], in_=bank[:])
+
+        def load_keys_values(kv):
+            b, g = divmod(kv, KV_HEADS)
+            k_rows = loads.tile([P, BLOCKS * HEAD_DIM], BF16, tag="k_rows")
+            v_rows = loads.tile([P, PACK, SLOT_PASSES * HEAD_DIM], BF16, tag="v_rows")
+            for c in range(SLOT_PASSES):
+                slots = slice(c * K_PASS, (c + 1) * K_PASS)
+                nc.sync.dma_start(
+                    out=k_rows[:, c * K_PASS : (c + 1) * K_PASS].rearrange("p (t d) -> p t d", t=PACK),
+                    in_=k_mem[b, slots, g, :].rearrange("(p t) d -> p t d", t=PACK),
+                )
+                nc.sync.dma_start(
+                    out=v_rows[:, :, c * HEAD_DIM : (c + 1) * HEAD_DIM],
+                    in_=v_mem[b, slots, g, :].rearrange("(p t) d -> p t d", t=PACK),
+                )
+            return k_rows, v_rows
+
+        def prepare_keys_values(kv, k_rows, v_rows):
+            bank = psum_misc.tile([P, BLOCKS, P], BF16, tag="misc")
+            transpose_blocks(bank, k_rows)
+            nc.scalar.copy(out=k_t[:, kv, :], in_=bank[:].rearrange("p x m -> p (x m)"))
+            v_grouped = work.tile([P, SLOT_PASSES * HEAD_DIM, PACK], BF16, tag="v_grouped", align_bytes=64)
+            nc.vector.tensor_copy(
+                out=v_grouped[:].rearrange("p (x i) t -> p x t i", i=4),
+                in_=v_rows[:].rearrange("p t (x i) -> p x t i", i=4),
+            )
+            quantise(v_codes[:, kv, :], v_scales[:, kv, :], v_grouped[:].rearrange("p x t -> p (x t)"))
+
+        def load_wo(pair):
+            wo_rows = loads.tile([P, 2, FEATURES], BF16, tag="wo_rows")
+            nc.sync.dma_start(
+                out=wo_rows[:], in_=Wo[pair * WO_ROWS : (pair + 1) * WO_ROWS, :].rearrange("(x p) a -> p x a", p=P)
+            )
+            return wo_rows
+
+        def prepare_wo(pair, wo_rows, c):
+            bank = psum_misc.tile([P, 2, WO_ROWS], F32, tag="misc")
+            for u in range(2):
+                first = (2 * c + u) * P
+                for x in range(2):
+                    nc.tensor.transpose(
+                        out=bank[:, u, x * P : (x + 1) * P],
+                        in_=wo_rows[:, x, :].bitcast(F32)[:, first : first + P],
+                        identity=ident_f32[:],
+                    )
+            wo_grouped = work.tile([P, WO_ROWS * PACK], BF16, tag="wo_grouped", align_bytes=64)
+            copy = nc.scalar.copy if c % 2 == 0 else nc.vector.tensor_copy
+            copy(
+                out=wo_grouped[:].bitcast(F32).rearrange("p (r u) -> p r u", u=2),
+                in_=bank[:].rearrange("p u r -> p r u"),
+            )
+            rows = slice(pair * WO_ROWS, (pair + 1) * WO_ROWS)
+            quantise(wo_codes[:, c, rows], wo_scales[:, c, rows], wo_grouped[:])
+
+        def softmax_numerator(kv, query_tile, head, row_sum):
+            scores = []
+            tops = small.tile([P, SLOT_PASSES], F32, tag="tops")
+            for c in range(SLOT_PASSES):
+                s = psum_scores.tile([P, K_PASS], F32, tag="s")
+                nc.tensor.matmul(
+                    out=s[:],
+                    lhsT=q_t[:, query_tile, head, :],
+                    rhs=k_t[:, kv, c * K_PASS : (c + 1) * K_PASS],
+                    start=True,
+                    stop=True,
+                )
+                nc.vector.tensor_reduce(out=tops[:, c : c + 1], in_=s[:], axis=ALONG_ROW, op=ALU.max)
+                scores.append(s)
+            shift = small.tile([P, 1], F32, tag="shift")
+            nc.vector.tensor_scalar(
+                out=shift[:], in0=tops[:, 0:1], scalar1=tops[:, 1:2], scalar2=-SCORE_FACTOR, op0=ALU.max, op1=ALU.mult
+            )
+            e_rows = work.tile([P, SLOTS], BF16, tag="e_rows")
+            for c in range(SLOT_PASSES):
+                nc.scalar.activation(
+                    out=e_rows[:, c * K_PASS : (c + 1) * K_PASS],
+                    in_=scores[c][:],
+                    func=EXP,
+                    bias=shift[:],
+                    scale=SCORE_FACTOR,
+                    accum_out=row_sum[:, c : c + 1],
+                )
+            bank = psum_et.tile([P, BLOCKS, P], BF16, tag="et")
+            transpose_blocks(bank, e_rows)
+            e_grouped = group_words(nc.scalar.copy, bank)
+            e_codes = codes_pool.tile([P, SLOT_PASSES * P], U32, tag="e_codes", align_bytes=64)
+            e_scales = codes_pool.tile([P, SLOT_PASSES * P], U8, tag="e_scales", align_bytes=64)
+            quantise(e_codes[:], e_scales[:], e_grouped)
+            return e_codes, e_scales
+
+        def attend(b, query_tile, g, a_rows):
+            kv = b * KV_HEADS + g
+            row_sums = small.tile([P, GROUP, SLOT_PASSES], F32, tag="row_sums")
+            e_mx = [
+                softmax_numerator(kv, query_tile, GROUP * g + j, row_sums[:, j, :]) for j in range(GROUP)
+            ]
+            o = psum_o.tile([P, GROUP, HEAD_DIM], F32, tag="o")
+            for j in range(GROUP):
+                e_codes, e_scales = e_mx[j]
+                for c in range(SLOT_PASSES):
+                    cols = slice(c * P, (c + 1) * P)
+                    nc.tensor.matmul_mx(
+                        out=o[:, j, :],
+                        lhsT=e_codes[:, cols].bitcast(FP8X4),
+                        lhsT_scale=e_scales[:, cols],
+                        rhs=v_codes[:, kv, cols].bitcast(FP8X4),
+                        rhs_scale=v_scales[:, kv, cols],
+                        start=(c == 0),
+                        stop=(c == SLOT_PASSES - 1),
+                    )
+            total = small.tile([P, GROUP], F32, tag="total")
+            nc.vector.tensor_reduce(out=total[:], in_=row_sums[:], axis=ALONG_ROW, op=ALU.add)
+            inverse = small.tile([P, GROUP], F32, tag="inverse")
+            nc.vector.reciprocal(out=inverse[:], in_=total[:])
+            nc.vector.tensor_tensor(
+                out=a_rows[:, g * GROUP * HEAD_DIM : (g + 1) * GROUP * HEAD_DIM].rearrange(
+                    "q (w j i) -> q j w i", w=2, j=GROUP
+                ),
+                in0=o[:].rearrange("q j (i w) -> q j w i", w=2),
+                in1=inverse[:].unsqueeze(2).unsqueeze(3).broadcast_to([P, GROUP, 2, HEAD_DIM // 2]),
+                op=ALU.mult,
+            )
+
+        def quantise_a(tile_index, a_rows, half):
+            bank = psum_misc.tile([P, BLOCKS, P], BF16, tag="misc")
+            transpose_blocks(bank, a_rows[:, half * BLOCKS * P : (half + 1) * BLOCKS * P])
+            a_grouped = group_words(nc.vector.tensor_copy, bank)
+            cols = slice(half * 2 * P, (half + 1) * 2 * P)
+            quantise(a_codes[:, tile_index, cols], a_scales[:, tile_index, cols], a_grouped)
+
+        def project(tile_index, block):
+            b, query_tile = divmod(tile_index, QUERY_TILES)
+            cols = slice(block * OUT_COLS, (block + 1) * OUT_COLS)
+            acc = psum_misc.tile([P, OUT_COLS], F32, tag="misc")
+            for c in range(FEATURE_PASSES):
+                nc.tensor.matmul_mx(
+                    out=acc[:],
+                    lhsT=a_codes[:, tile_index, c * P : (c + 1) * P].bitcast(FP8X4),
+                    lhsT_scale=a_scales[:, tile_index, c * P : (c + 1) * P],
+                    rhs=wo_codes[:, c, cols].bitcast(FP8X4),
+                    rhs_scale=wo_scales[:, c, cols],
+                    start=(c == 0),
+                    stop=(c == FEATURE_PASSES - 1),
+                )
+            result = work.tile([P, OUT_COLS], F32, tag="result")
+            copy = nc.vector.tensor_copy if block % 2 == 0 else nc.scalar.copy
+            copy(out=result[:], in_=acc[:])
+            nc.sync.dma_start(out=out[b, query_tile * P : (query_tile + 1) * P, cols], in_=result[:])
+
+        for query_tile in range(QUERY_TILES):
+            prepare_queries(query_tile)
+
+        for tile_index in range(BATCH * QUERY_TILES):
+            b, query_tile = divmod(tile_index, QUERY_TILES)
+            a_rows = work.tile([P, FEATURES], BF16, tag="a_rows", bufs=2)
+            for g in range(KV_HEADS):
+                step = query_tile * KV_HEADS + g
+                if query_tile == 0:
+                    kv = b * KV_HEADS + g
+                    k_rows, v_rows = load_keys_values(kv)
+                    prepare_keys_values(kv, k_rows, v_rows)
+                attend(b, query_tile, g, a_rows)
+                if g % (KV_HEADS // 2) == KV_HEADS // 2 - 1:
+                    quantise_a(tile_index, a_rows, g // (KV_HEADS // 2))
+                if b == 0:
+                    pair, half = divmod(step, 2)
+                    if half == 0:
+                        wo_rows = load_wo(pair)
+                    for c in (2 * half, 2 * half + 1):
+                        prepare_wo(pair, wo_rows, c)
+                elif step < (BATCH * QUERY_TILES - 1) * OUT_BLOCKS:
+                    project(step // OUT_BLOCKS, step % OUT_BLOCKS)
+        for block in range(OUT_BLOCKS):
+            project(BATCH * QUERY_TILES - 1, block)

@@ -28,12 +28,28 @@ MODEL = 2048
 SCORE_FACTOR = 0.5
 
 QUERY_TILES = QUERIES // P
+ROW_TILES = BATCH * QUERY_TILES
+KV = BATCH * KV_HEADS
 SLOT_PASSES = SLOTS // K_PASS
 FEATURE_PASSES = FEATURES // K_PASS
 BLOCKS = 2 * PACK
 OUT_COLS = 512
 OUT_BLOCKS = MODEL // OUT_COLS
 WO_ROWS = 2 * P
+WO_UNITS = (MODEL // WO_ROWS) * FEATURE_PASSES
+
+STEPS = ROW_TILES * KV_HEADS
+HEAD_TILES = STEPS * GROUP
+EXP_LAG = 1
+TRANSPOSE_LAG = 2
+QUANTISE_LAG = 3
+VALUES_LAG = QUANTISE_LAG + GROUP
+A_STEPS = KV_HEADS // 2
+A_PERIOD = A_STEPS * GROUP
+A_LAG = VALUES_LAG + (A_STEPS - 1) * GROUP + 1
+PROJECT_LAG = A_LAG + (2 * QUERY_TILES - 1) * A_PERIOD + 3
+SECOND_QUERIES_TICK = 4
+LAST_TICK = A_LAG + (2 * ROW_TILES - 1) * A_PERIOD + 1
 
 FLOPS = 2 * (2 * BATCH * HEADS * QUERIES * SLOTS * HEAD_DIM) + 2 * BATCH * QUERIES * FEATURES * MODEL
 
@@ -47,9 +63,9 @@ def tile_qwen2dymemdecoderlayer_pa_kernel(tc, q_pos, k_mem, v_mem, Wo, out):
         codes_pool = ctx.enter_context(tc.tile_pool(name="codes", bufs=6))
         small = ctx.enter_context(tc.tile_pool(name="small", bufs=6))
         psum_scores = ctx.enter_context(tc.psum_pool(name="psum_scores", bufs=4))
-        psum_et = ctx.enter_context(tc.psum_pool(name="psum_et", bufs=1))
-        psum_o = ctx.enter_context(tc.psum_pool(name="psum_o", bufs=1))
+        psum_et = ctx.enter_context(tc.psum_pool(name="psum_et", bufs=2))
         psum_misc = ctx.enter_context(tc.psum_pool(name="psum_misc", bufs=2))
+        ctx.enter_context(tc.manual_schedule())
 
         ident_bf16 = keep.tile([P, P], BF16)
         masks.make_identity(nc, ident_bf16[:])
@@ -57,13 +73,17 @@ def tile_qwen2dymemdecoderlayer_pa_kernel(tc, q_pos, k_mem, v_mem, Wo, out):
         masks.make_identity(nc, ident_f32[:])
 
         q_t = keep.tile([P, QUERY_TILES, HEADS, P], BF16)
-        k_t = keep.tile([P, BATCH * KV_HEADS, SLOTS], BF16)
-        v_codes = keep.tile([P, BATCH * KV_HEADS, SLOT_PASSES * HEAD_DIM], U32, align_bytes=64)
-        v_scales = keep.tile([P, BATCH * KV_HEADS, SLOT_PASSES * HEAD_DIM], U8, align_bytes=64)
+        k_t = keep.tile([P, KV, SLOTS], BF16)
+        v_codes = keep.tile([P, KV, SLOT_PASSES * HEAD_DIM], U32, align_bytes=64)
+        v_scales = keep.tile([P, KV, SLOT_PASSES * HEAD_DIM], U8, align_bytes=64)
         wo_codes = keep.tile([P, FEATURE_PASSES, MODEL], U32, align_bytes=64)
         wo_scales = keep.tile([P, FEATURE_PASSES, MODEL], U8, align_bytes=64)
-        a_codes = keep.tile([P, BATCH * QUERY_TILES, FEATURE_PASSES * P], U32, align_bytes=64)
-        a_scales = keep.tile([P, BATCH * QUERY_TILES, FEATURE_PASSES * P], U8, align_bytes=64)
+        a_codes = keep.tile([P, ROW_TILES, FEATURE_PASSES * P], U32, align_bytes=64)
+        a_scales = keep.tile([P, ROW_TILES, FEATURE_PASSES * P], U8, align_bytes=64)
+
+        q_rows, k_rows, v_rows, v_grouped, wo_rows, wo_grouped = {}, {}, {}, {}, {}, {}
+        score_banks, shifts, row_sums, e_rows, e_grouped, e_mx, o_banks = {}, {}, {}, {}, {}, {}, {}
+        a_rows, a_grouped = {}, {}
 
         def quantise(codes, scales, grouped):
             nc.vector.quantize_mx(out=codes.bitcast(FP8X4), scales=scales, in_=grouped)
@@ -77,114 +97,146 @@ def tile_qwen2dymemdecoderlayer_pa_kernel(tc, q_pos, k_mem, v_mem, Wo, out):
             copy(out=grouped[:], in_=bank[:].rearrange("p (c t) r -> p c r t", t=PACK))
             return grouped[:].rearrange("p c r t -> p (c r t)")
 
-        def prepare_queries(query_tile):
-            q_rows = loads.tile([P, HEADS * HEAD_DIM], BF16, tag="q_rows")
+        def load_queries(query_tile):
+            rows = loads.tile([P, HEADS * HEAD_DIM], BF16, tag="q_rows", bufs=2)
             nc.sync.dma_start(
-                out=q_rows[:], in_=q_pos[query_tile * P : (query_tile + 1) * P].rearrange("q h d -> q (h d)")
+                out=rows[:], in_=q_pos[query_tile * P : (query_tile + 1) * P].rearrange("q h d -> q (h d)")
             )
+            q_rows[query_tile] = rows
+
+        def transpose_queries(query_tile):
             for half in range(HEADS // BLOCKS):
                 bank = psum_misc.tile([P, BLOCKS, P], BF16, tag="misc")
-                transpose_blocks(bank, q_rows[:, half * BLOCKS * P : (half + 1) * BLOCKS * P])
+                transpose_blocks(bank, q_rows[query_tile][:, half * BLOCKS * P : (half + 1) * BLOCKS * P])
                 nc.vector.tensor_copy(out=q_t[:, query_tile, half * BLOCKS : (half + 1) * BLOCKS, :], in_=bank[:])
 
-        def load_keys_values(kv):
+        def load_keys(kv):
             b, g = divmod(kv, KV_HEADS)
-            k_rows = loads.tile([P, BLOCKS * HEAD_DIM], BF16, tag="k_rows")
-            v_rows = loads.tile([P, PACK, SLOT_PASSES * HEAD_DIM], BF16, tag="v_rows")
+            rows = loads.tile([P, BLOCKS * HEAD_DIM], BF16, tag="k_rows")
             for c in range(SLOT_PASSES):
-                slots = slice(c * K_PASS, (c + 1) * K_PASS)
                 nc.sync.dma_start(
-                    out=k_rows[:, c * K_PASS : (c + 1) * K_PASS].rearrange("p (t d) -> p t d", t=PACK),
-                    in_=k_mem[b, slots, g, :].rearrange("(p t) d -> p t d", t=PACK),
+                    out=rows[:, c * K_PASS : (c + 1) * K_PASS].rearrange("p (t d) -> p t d", t=PACK),
+                    in_=k_mem[b, c * K_PASS : (c + 1) * K_PASS, g, :].rearrange("(p t) d -> p t d", t=PACK),
                 )
-                nc.sync.dma_start(
-                    out=v_rows[:, :, c * HEAD_DIM : (c + 1) * HEAD_DIM],
-                    in_=v_mem[b, slots, g, :].rearrange("(p t) d -> p t d", t=PACK),
-                )
-            return k_rows, v_rows
+            k_rows[kv] = rows
 
-        def prepare_keys_values(kv, k_rows, v_rows):
+        def load_values(kv):
+            b, g = divmod(kv, KV_HEADS)
+            rows = loads.tile([P, PACK, SLOT_PASSES * HEAD_DIM], BF16, tag="v_rows")
+            for c in range(SLOT_PASSES):
+                nc.sync.dma_start(
+                    out=rows[:, :, c * HEAD_DIM : (c + 1) * HEAD_DIM],
+                    in_=v_mem[b, c * K_PASS : (c + 1) * K_PASS, g, :].rearrange("(p t) d -> p t d", t=PACK),
+                )
+            v_rows[kv] = rows
+
+        def transpose_keys(kv):
             bank = psum_misc.tile([P, BLOCKS, P], BF16, tag="misc")
-            transpose_blocks(bank, k_rows)
+            transpose_blocks(bank, k_rows[kv])
             nc.scalar.copy(out=k_t[:, kv, :], in_=bank[:].rearrange("p x m -> p (x m)"))
-            v_grouped = work.tile([P, SLOT_PASSES * HEAD_DIM, PACK], BF16, tag="v_grouped", align_bytes=64)
+
+        def group_values(kv):
+            grouped = work.tile([P, SLOT_PASSES * HEAD_DIM, PACK], BF16, tag="v_grouped", align_bytes=64)
             nc.vector.tensor_copy(
-                out=v_grouped[:].rearrange("p (x i) t -> p x t i", i=4),
-                in_=v_rows[:].rearrange("p t (x i) -> p x t i", i=4),
+                out=grouped[:].rearrange("p (x i) t -> p x t i", i=4),
+                in_=v_rows[kv][:].rearrange("p t (x i) -> p x t i", i=4),
             )
-            quantise(v_codes[:, kv, :], v_scales[:, kv, :], v_grouped[:].rearrange("p x t -> p (x t)"))
+            v_grouped[kv] = grouped
+
+        def quantise_values(kv):
+            quantise(v_codes[:, kv, :], v_scales[:, kv, :], v_grouped[kv][:].rearrange("p x t -> p (x t)"))
 
         def load_wo(pair):
-            wo_rows = loads.tile([P, 2, FEATURES], BF16, tag="wo_rows")
+            rows = loads.tile([P, 2, FEATURES], BF16, tag="wo_rows")
             nc.sync.dma_start(
-                out=wo_rows[:], in_=Wo[pair * WO_ROWS : (pair + 1) * WO_ROWS, :].rearrange("(x p) a -> p x a", p=P)
+                out=rows[:], in_=Wo[pair * WO_ROWS : (pair + 1) * WO_ROWS, :].rearrange("(x p) a -> p x a", p=P)
             )
-            return wo_rows
+            wo_rows[pair] = rows
 
-        def prepare_wo(pair, wo_rows, c):
+        def transpose_wo(unit):
+            pair, c = divmod(unit, FEATURE_PASSES)
             bank = psum_misc.tile([P, 2, WO_ROWS], F32, tag="misc")
             for u in range(2):
                 first = (2 * c + u) * P
                 for x in range(2):
                     nc.tensor.transpose(
                         out=bank[:, u, x * P : (x + 1) * P],
-                        in_=wo_rows[:, x, :].bitcast(F32)[:, first : first + P],
+                        in_=wo_rows[pair][:, x, :].bitcast(F32)[:, first : first + P],
                         identity=ident_f32[:],
                     )
-            wo_grouped = work.tile([P, WO_ROWS * PACK], BF16, tag="wo_grouped", align_bytes=64)
+            grouped = work.tile([P, WO_ROWS * PACK], BF16, tag="wo_grouped", align_bytes=64)
             copy = nc.scalar.copy if c % 2 == 0 else nc.vector.tensor_copy
             copy(
-                out=wo_grouped[:].bitcast(F32).rearrange("p (r u) -> p r u", u=2),
+                out=grouped[:].bitcast(F32).rearrange("p (r u) -> p r u", u=2),
                 in_=bank[:].rearrange("p u r -> p r u"),
             )
-            rows = slice(pair * WO_ROWS, (pair + 1) * WO_ROWS)
-            quantise(wo_codes[:, c, rows], wo_scales[:, c, rows], wo_grouped[:])
+            wo_grouped[unit] = grouped
 
-        def softmax_numerator(kv, query_tile, head, row_sum):
-            scores = []
+        def quantise_wo(unit):
+            pair, c = divmod(unit, FEATURE_PASSES)
+            rows = slice(pair * WO_ROWS, (pair + 1) * WO_ROWS)
+            quantise(wo_codes[:, c, rows], wo_scales[:, c, rows], wo_grouped[unit][:])
+
+        def place(i):
+            step, j = divmod(i, GROUP)
+            tile_index, g = divmod(step, KV_HEADS)
+            return step, j, tile_index, (tile_index // QUERY_TILES) * KV_HEADS + g, g
+
+
+        def scores(i):
+            step, j, tile_index, kv, g = place(i)
+            score_banks[i] = []
             tops = small.tile([P, SLOT_PASSES], F32, tag="tops")
             for c in range(SLOT_PASSES):
                 s = psum_scores.tile([P, K_PASS], F32, tag="s")
                 nc.tensor.matmul(
                     out=s[:],
-                    lhsT=q_t[:, query_tile, head, :],
+                    lhsT=q_t[:, tile_index % QUERY_TILES, GROUP * g + j, :],
                     rhs=k_t[:, kv, c * K_PASS : (c + 1) * K_PASS],
                     start=True,
                     stop=True,
                 )
                 nc.vector.tensor_reduce(out=tops[:, c : c + 1], in_=s[:], axis=ALONG_ROW, op=ALU.max)
-                scores.append(s)
+                score_banks[i].append(s)
             shift = small.tile([P, 1], F32, tag="shift")
             nc.vector.tensor_scalar(
                 out=shift[:], in0=tops[:, 0:1], scalar1=tops[:, 1:2], scalar2=-SCORE_FACTOR, op0=ALU.max, op1=ALU.mult
             )
-            e_rows = work.tile([P, SLOTS], BF16, tag="e_rows")
+            shifts[i] = shift
+
+        def exponentials(i):
+            step, j, tile_index, kv, g = place(i)
+            if j == 0:
+                sums = small.tile([P, GROUP, SLOT_PASSES], F32, tag="sums")
+                row_sums[step] = sums
+            e = work.tile([P, SLOTS], BF16, tag="e")
             for c in range(SLOT_PASSES):
                 nc.scalar.activation(
-                    out=e_rows[:, c * K_PASS : (c + 1) * K_PASS],
-                    in_=scores[c][:],
+                    out=e[:, c * K_PASS : (c + 1) * K_PASS],
+                    in_=score_banks[i][c][:],
                     func=EXP,
-                    bias=shift[:],
+                    bias=shifts[i][:],
                     scale=SCORE_FACTOR,
-                    accum_out=row_sum[:, c : c + 1],
+                    accum_out=row_sums[step][:, j, c : c + 1],
                 )
+            e_rows[i] = e
+
+        def transpose_e(i):
             bank = psum_et.tile([P, BLOCKS, P], BF16, tag="et")
-            transpose_blocks(bank, e_rows)
-            e_grouped = group_words(nc.scalar.copy, bank)
+            transpose_blocks(bank, e_rows[i])
+            e_grouped[i] = group_words(nc.scalar.copy, bank)
+
+        def quantise_e(i):
             e_codes = codes_pool.tile([P, SLOT_PASSES * P], U32, tag="e_codes", align_bytes=64)
             e_scales = codes_pool.tile([P, SLOT_PASSES * P], U8, tag="e_scales", align_bytes=64)
-            quantise(e_codes[:], e_scales[:], e_grouped)
-            return e_codes, e_scales
+            quantise(e_codes[:], e_scales[:], e_grouped[i])
+            e_mx[i] = (e_codes, e_scales)
 
-        def attend(b, query_tile, g, a_rows):
-            kv = b * KV_HEADS + g
-            row_sums = small.tile([P, GROUP, SLOT_PASSES], F32, tag="row_sums")
-            e_mx = [
-                softmax_numerator(kv, query_tile, GROUP * g + j, row_sums[:, j, :]) for j in range(GROUP)
-            ]
-            o = psum_o.tile([P, GROUP, HEAD_DIM], F32, tag="o")
+        def weigh_values(step):
+            kv = place(GROUP * step)[3]
+            o = psum_misc.tile([P, GROUP, HEAD_DIM], F32, tag="misc")
             for j in range(GROUP):
-                e_codes, e_scales = e_mx[j]
+                e_codes, e_scales = e_mx[GROUP * step + j]
                 for c in range(SLOT_PASSES):
                     cols = slice(c * P, (c + 1) * P)
                     nc.tensor.matmul_mx(
@@ -196,27 +248,39 @@ def tile_qwen2dymemdecoderlayer_pa_kernel(tc, q_pos, k_mem, v_mem, Wo, out):
                         start=(c == 0),
                         stop=(c == SLOT_PASSES - 1),
                     )
+            o_banks[step] = o
+
+        def normalise(step):
+            tile_index, g = divmod(step, KV_HEADS)
+            if g == 0:
+                rows = work.tile([P, FEATURES], BF16, tag="a", bufs=2)
+                a_rows[tile_index] = rows
             total = small.tile([P, GROUP], F32, tag="total")
-            nc.vector.tensor_reduce(out=total[:], in_=row_sums[:], axis=ALONG_ROW, op=ALU.add)
+            nc.vector.tensor_reduce(out=total[:], in_=row_sums[step][:], axis=ALONG_ROW, op=ALU.add)
             inverse = small.tile([P, GROUP], F32, tag="inverse")
             nc.vector.reciprocal(out=inverse[:], in_=total[:])
             nc.vector.tensor_tensor(
-                out=a_rows[:, g * GROUP * HEAD_DIM : (g + 1) * GROUP * HEAD_DIM].rearrange(
+                out=a_rows[tile_index][:, g * GROUP * HEAD_DIM : (g + 1) * GROUP * HEAD_DIM].rearrange(
                     "q (w j i) -> q j w i", w=2, j=GROUP
                 ),
-                in0=o[:].rearrange("q j (i w) -> q j w i", w=2),
+                in0=o_banks[step][:].rearrange("q j (i w) -> q j w i", w=2),
                 in1=inverse[:].unsqueeze(2).unsqueeze(3).broadcast_to([P, GROUP, 2, HEAD_DIM // 2]),
                 op=ALU.mult,
             )
 
-        def quantise_a(tile_index, a_rows, half):
+        def transpose_a(half_index):
+            tile_index, half = divmod(half_index, 2)
             bank = psum_misc.tile([P, BLOCKS, P], BF16, tag="misc")
-            transpose_blocks(bank, a_rows[:, half * BLOCKS * P : (half + 1) * BLOCKS * P])
-            a_grouped = group_words(nc.vector.tensor_copy, bank)
-            cols = slice(half * 2 * P, (half + 1) * 2 * P)
-            quantise(a_codes[:, tile_index, cols], a_scales[:, tile_index, cols], a_grouped)
+            transpose_blocks(bank, a_rows[tile_index][:, half * BLOCKS * P : (half + 1) * BLOCKS * P])
+            a_grouped[half_index] = group_words(nc.vector.tensor_copy, bank)
 
-        def project(tile_index, block):
+        def quantise_a(half_index):
+            tile_index, half = divmod(half_index, 2)
+            cols = slice(half * 2 * P, (half + 1) * 2 * P)
+            quantise(a_codes[:, tile_index, cols], a_scales[:, tile_index, cols], a_grouped[half_index])
+
+        def project(block_index):
+            tile_index, block = divmod(block_index, OUT_BLOCKS)
             b, query_tile = divmod(tile_index, QUERY_TILES)
             cols = slice(block * OUT_COLS, (block + 1) * OUT_COLS)
             acc = psum_misc.tile([P, OUT_COLS], F32, tag="misc")
@@ -235,28 +299,61 @@ def tile_qwen2dymemdecoderlayer_pa_kernel(tc, q_pos, k_mem, v_mem, Wo, out):
             copy(out=result[:], in_=acc[:])
             nc.sync.dma_start(out=out[b, query_tile * P : (query_tile + 1) * P, cols], in_=result[:])
 
-        for query_tile in range(QUERY_TILES):
-            prepare_queries(query_tile)
+        load_keys(0)
+        load_queries(0)
+        load_values(0)
+        for kv in (1, 2):
+            load_keys(kv)
+            load_values(kv)
+        load_queries(1)
+        for pair in (0, 1):
+            load_wo(pair)
+        transpose_queries(0)
+        transpose_keys(0)
+        group_values(0)
+        quantise_values(0)
 
-        for tile_index in range(BATCH * QUERY_TILES):
-            b, query_tile = divmod(tile_index, QUERY_TILES)
-            a_rows = work.tile([P, FEATURES], BF16, tag="a_rows", bufs=2)
-            for g in range(KV_HEADS):
-                step = query_tile * KV_HEADS + g
-                if query_tile == 0:
-                    kv = b * KV_HEADS + g
-                    k_rows, v_rows = load_keys_values(kv)
-                    prepare_keys_values(kv, k_rows, v_rows)
-                attend(b, query_tile, g, a_rows)
-                if g % (KV_HEADS // 2) == KV_HEADS // 2 - 1:
-                    quantise_a(tile_index, a_rows, g // (KV_HEADS // 2))
-                if b == 0:
-                    pair, half = divmod(step, 2)
-                    if half == 0:
-                        wo_rows = load_wo(pair)
-                    for c in (2 * half, 2 * half + 1):
-                        prepare_wo(pair, wo_rows, c)
-                elif step < (BATCH * QUERY_TILES - 1) * OUT_BLOCKS:
-                    project(step // OUT_BLOCKS, step % OUT_BLOCKS)
+        for tick in range(LAST_TICK + 1):
+            if tick < HEAD_TILES:
+                scores(tick)
+            if 0 <= tick - EXP_LAG < HEAD_TILES:
+                exponentials(tick - EXP_LAG)
+            if 0 <= tick - TRANSPOSE_LAG < HEAD_TILES:
+                transpose_e(tick - TRANSPOSE_LAG)
+            if 0 <= tick - QUANTISE_LAG < HEAD_TILES:
+                quantise_e(tick - QUANTISE_LAG)
+            step, rest = divmod(tick - VALUES_LAG, GROUP)
+            if rest == 0 and 0 <= step < STEPS:
+                weigh_values(step)
+                normalise(step)
+            block_index, rest = divmod(tick - PROJECT_LAG, 2)
+            if rest == 0 and 0 <= block_index < (ROW_TILES - 1) * OUT_BLOCKS:
+                project(block_index)
+            half_index, rest = divmod(tick - A_LAG, A_PERIOD)
+            if rest == 0 and half_index >= 0:
+                transpose_a(half_index)
+            if rest == 1 and half_index >= 0:
+                quantise_a(half_index)
+            if 0 <= tick - 1 < WO_UNITS:
+                quantise_wo(tick - 1)
+            if tick < WO_UNITS:
+                transpose_wo(tick)
+                pair, c = divmod(tick, FEATURE_PASSES)
+                if c == 0 and pair + 2 < MODEL // WO_ROWS:
+                    load_wo(pair + 2)
+            kv, rest = divmod(tick, 2)
+            kv += 1
+            if kv < KV:
+                if rest == 0:
+                    transpose_keys(kv)
+                    group_values(kv)
+                    if kv + 2 < KV:
+                        load_keys(kv + 2)
+                        load_values(kv + 2)
+                else:
+                    quantise_values(kv)
+            if tick == SECOND_QUERIES_TICK:
+                transpose_queries(1)
+
         for block in range(OUT_BLOCKS):
-            project(BATCH * QUERY_TILES - 1, block)
+            project((ROW_TILES - 1) * OUT_BLOCKS + block)

@@ -44,12 +44,14 @@ EXP_LAG = 1
 TRANSPOSE_LAG = 2
 QUANTISE_LAG = 3
 VALUES_LAG = QUANTISE_LAG + GROUP
-A_STEPS = KV_HEADS // 2
+A_STEPS = K_PASS // (GROUP * HEAD_DIM)
 A_PERIOD = A_STEPS * GROUP
-A_LAG = VALUES_LAG + (A_STEPS - 1) * GROUP + 1
-PROJECT_LAG = A_LAG + (2 * QUERY_TILES - 1) * A_PERIOD + 3
+A_LAG = VALUES_LAG + (A_STEPS - 1) * GROUP + 2
+PROJECT_LAG = A_LAG + (QUERY_TILES * FEATURE_PASSES - 1) * A_PERIOD + 2
+WO_LAG = 4
+VECTOR_SHARE = 8
 SECOND_QUERIES_TICK = 4
-LAST_TICK = A_LAG + (2 * ROW_TILES - 1) * A_PERIOD + 1
+LAST_TICK = A_LAG + (ROW_TILES * FEATURE_PASSES - 1) * A_PERIOD + 1
 
 FLOPS = 2 * (2 * BATCH * HEADS * QUERIES * SLOTS * HEAD_DIM) + 2 * BATCH * QUERIES * FEATURES * MODEL
 
@@ -89,11 +91,10 @@ def tile_qwen2dymemdecoderlayer_pa_kernel(tc, q_pos, k_mem, v_mem, Wo, out):
             nc.vector.quantize_mx(out=codes.bitcast(FP8X4), scales=scales, in_=grouped)
 
         def transpose_blocks(bank, rows):
-            for x in range(BLOCKS):
+            for x in range(rows.shape[1] // P):
                 nc.tensor.transpose(out=bank[:, x, :], in_=rows[:, x * P : (x + 1) * P], identity=ident_bf16[:])
 
-        def group_words(copy, bank):
-            grouped = work.tile([P, 2, P, PACK], BF16, tag="grouped", align_bytes=64)
+        def group_words(copy, bank, grouped):
             copy(out=grouped[:], in_=bank[:].rearrange("p (c t) r -> p c r t", t=PACK))
             return grouped[:].rearrange("p c r t -> p (c r t)")
 
@@ -122,29 +123,26 @@ def tile_qwen2dymemdecoderlayer_pa_kernel(tc, q_pos, k_mem, v_mem, Wo, out):
 
         def load_values(kv):
             b, g = divmod(kv, KV_HEADS)
-            rows = loads.tile([P, PACK, SLOT_PASSES * HEAD_DIM], BF16, tag="v_rows")
+            rows = loads.tile([P, SLOT_PASSES, PACK, HEAD_DIM], BF16, tag="v_rows")
             for c in range(SLOT_PASSES):
                 nc.sync.dma_start(
-                    out=rows[:, :, c * HEAD_DIM : (c + 1) * HEAD_DIM],
+                    out=rows[:, c, :, :],
                     in_=v_mem[b, c * K_PASS : (c + 1) * K_PASS, g, :].rearrange("(p t) d -> p t d", t=PACK),
                 )
             v_rows[kv] = rows
 
         def transpose_keys(kv):
-            bank = psum_misc.tile([P, BLOCKS, P], BF16, tag="misc")
+            bank = psum_et.tile([P, BLOCKS, P], BF16, tag="et")
             transpose_blocks(bank, k_rows[kv])
             nc.scalar.copy(out=k_t[:, kv, :], in_=bank[:].rearrange("p x m -> p (x m)"))
 
         def group_values(kv):
-            grouped = work.tile([P, SLOT_PASSES * HEAD_DIM, PACK], BF16, tag="v_grouped", align_bytes=64)
-            nc.vector.tensor_copy(
-                out=grouped[:].rearrange("p (x i) t -> p x t i", i=4),
-                in_=v_rows[kv][:].rearrange("p t (x i) -> p x t i", i=4),
-            )
+            grouped = work.tile([P, SLOT_PASSES, HEAD_DIM, PACK], BF16, tag="v_grouped", align_bytes=64)
+            nc.vector.tensor_copy(out=grouped[:], in_=v_rows[kv][:].rearrange("p c t d -> p c d t"))
             v_grouped[kv] = grouped
 
         def quantise_values(kv):
-            quantise(v_codes[:, kv, :], v_scales[:, kv, :], v_grouped[kv][:].rearrange("p x t -> p (x t)"))
+            quantise(v_codes[:, kv, :], v_scales[:, kv, :], v_grouped[kv][:].rearrange("p c d t -> p (c d t)"))
 
         def load_wo(pair):
             rows = loads.tile([P, 2, FEATURES], BF16, tag="wo_rows")
@@ -224,7 +222,9 @@ def tile_qwen2dymemdecoderlayer_pa_kernel(tc, q_pos, k_mem, v_mem, Wo, out):
         def transpose_e(i):
             bank = psum_et.tile([P, BLOCKS, P], BF16, tag="et")
             transpose_blocks(bank, e_rows[i])
-            e_grouped[i] = group_words(nc.scalar.copy, bank)
+            grouped = work.tile([P, SLOT_PASSES, P, PACK], BF16, tag="e_grouped", align_bytes=64)
+            to_vector = i >= HEAD_TILES // BATCH and i % VECTOR_SHARE == VECTOR_SHARE - 1
+            e_grouped[i] = group_words(nc.vector.tensor_copy if to_vector else nc.scalar.copy, bank, grouped)
 
         def quantise_e(i):
             e_codes = codes_pool.tile([P, SLOT_PASSES * P], U32, tag="e_codes", align_bytes=64)
@@ -268,16 +268,17 @@ def tile_qwen2dymemdecoderlayer_pa_kernel(tc, q_pos, k_mem, v_mem, Wo, out):
                 op=ALU.mult,
             )
 
-        def transpose_a(half_index):
-            tile_index, half = divmod(half_index, 2)
-            bank = psum_misc.tile([P, BLOCKS, P], BF16, tag="misc")
-            transpose_blocks(bank, a_rows[tile_index][:, half * BLOCKS * P : (half + 1) * BLOCKS * P])
-            a_grouped[half_index] = group_words(nc.vector.tensor_copy, bank)
+        def transpose_a(pass_index):
+            tile_index, c = divmod(pass_index, FEATURE_PASSES)
+            bank = psum_et.tile([P, PACK, P], BF16, tag="et")
+            transpose_blocks(bank, a_rows[tile_index][:, c * K_PASS : (c + 1) * K_PASS])
+            grouped = work.tile([P, 1, P, PACK], BF16, tag="a_grouped", align_bytes=64)
+            a_grouped[pass_index] = group_words(nc.vector.tensor_copy, bank, grouped)
 
-        def quantise_a(half_index):
-            tile_index, half = divmod(half_index, 2)
-            cols = slice(half * 2 * P, (half + 1) * 2 * P)
-            quantise(a_codes[:, tile_index, cols], a_scales[:, tile_index, cols], a_grouped[half_index])
+        def quantise_a(pass_index):
+            tile_index, c = divmod(pass_index, FEATURE_PASSES)
+            cols = slice(c * P, (c + 1) * P)
+            quantise(a_codes[:, tile_index, cols], a_scales[:, tile_index, cols], a_grouped[pass_index])
 
         def project(block_index):
             tile_index, block = divmod(block_index, OUT_BLOCKS)
@@ -301,17 +302,15 @@ def tile_qwen2dymemdecoderlayer_pa_kernel(tc, q_pos, k_mem, v_mem, Wo, out):
 
         load_keys(0)
         load_queries(0)
+        load_keys(1)
         load_values(0)
-        for kv in (1, 2):
-            load_keys(kv)
-            load_values(kv)
+        load_keys(2)
+        load_values(1)
         load_queries(1)
         for pair in (0, 1):
             load_wo(pair)
-        transpose_queries(0)
         transpose_keys(0)
-        group_values(0)
-        quantise_values(0)
+        transpose_queries(0)
 
         for tick in range(LAST_TICK + 1):
             if tick < HEAD_TILES:
@@ -329,29 +328,29 @@ def tile_qwen2dymemdecoderlayer_pa_kernel(tc, q_pos, k_mem, v_mem, Wo, out):
             block_index, rest = divmod(tick - PROJECT_LAG, 2)
             if rest == 0 and 0 <= block_index < (ROW_TILES - 1) * OUT_BLOCKS:
                 project(block_index)
-            half_index, rest = divmod(tick - A_LAG, A_PERIOD)
-            if rest == 0 and half_index >= 0:
-                transpose_a(half_index)
-            if rest == 1 and half_index >= 0:
-                quantise_a(half_index)
-            if 0 <= tick - 1 < WO_UNITS:
-                quantise_wo(tick - 1)
-            if tick < WO_UNITS:
-                transpose_wo(tick)
-                pair, c = divmod(tick, FEATURE_PASSES)
+            pass_index, rest = divmod(tick - A_LAG, A_PERIOD)
+            if rest == 0 and pass_index >= 0:
+                transpose_a(pass_index)
+            if rest == 1 and pass_index >= 0:
+                quantise_a(pass_index)
+            if 0 <= tick - WO_LAG - 1 < WO_UNITS:
+                quantise_wo(tick - WO_LAG - 1)
+            if 0 <= tick - WO_LAG < WO_UNITS:
+                transpose_wo(tick - WO_LAG)
+                pair, c = divmod(tick - WO_LAG, FEATURE_PASSES)
                 if c == 0 and pair + 2 < MODEL // WO_ROWS:
                     load_wo(pair + 2)
             kv, rest = divmod(tick, 2)
-            kv += 1
-            if kv < KV:
-                if rest == 0:
-                    transpose_keys(kv)
-                    group_values(kv)
-                    if kv + 2 < KV:
-                        load_keys(kv + 2)
-                        load_values(kv + 2)
-                else:
-                    quantise_values(kv)
+            if rest == 0 and kv + 1 < KV:
+                transpose_keys(kv + 1)
+                if kv + 3 < KV:
+                    load_keys(kv + 3)
+            if rest == 1 and kv < KV:
+                group_values(kv)
+                if kv + 2 < KV:
+                    load_values(kv + 2)
+            if rest == 0 and 0 <= kv - 1 < KV:
+                quantise_values(kv - 1)
             if tick == SECOND_QUERIES_TICK:
                 transpose_queries(1)
 

@@ -84,7 +84,7 @@ def tile_qwen2dymemdecoderlayer_pa_kernel(tc, q_pos, k_mem, v_mem, Wo, out):
         a_scales = keep.tile([P, ROW_TILES, FEATURE_PASSES * P], U8, align_bytes=64)
 
         q_rows, k_rows, v_rows, v_grouped, wo_rows, wo_grouped = {}, {}, {}, {}, {}, {}
-        score_banks, shifts, row_sums, e_rows, e_grouped, e_mx, o_banks = {}, {}, {}, {}, {}, {}, {}
+        score_banks, bank_tops, shifts, totals, inverses, row_sums, e_rows, e_grouped, e_mx, o_banks = {}, {}, {}, {}, {}, {}, {}, {}, {}, {}
         a_rows, a_grouped = {}, {}
 
         def quantise(codes, scales, grouped):
@@ -196,6 +196,10 @@ def tile_qwen2dymemdecoderlayer_pa_kernel(tc, q_pos, k_mem, v_mem, Wo, out):
                 )
                 nc.vector.tensor_reduce(out=tops[:, c : c + 1], in_=s[:], axis=ALONG_ROW, op=ALU.max)
                 score_banks[i].append(s)
+            bank_tops[i] = tops
+
+        def find_shift(i):
+            tops = bank_tops[i]
             shift = small.tile([P, 1], F32, tag="shift")
             nc.vector.tensor_scalar(
                 out=shift[:], in0=tops[:, 0:1], scalar1=tops[:, 1:2], scalar2=-SCORE_FACTOR, op0=ALU.max, op1=ALU.mult
@@ -250,21 +254,27 @@ def tile_qwen2dymemdecoderlayer_pa_kernel(tc, q_pos, k_mem, v_mem, Wo, out):
                     )
             o_banks[step] = o
 
+        def add_row_sums(step):
+            total = small.tile([P, GROUP], F32, tag="total")
+            nc.vector.tensor_reduce(out=total[:], in_=row_sums[step][:], axis=ALONG_ROW, op=ALU.add)
+            totals[step] = total
+
+        def invert_row_sums(step):
+            inverse = small.tile([P, GROUP], F32, tag="inverse")
+            nc.vector.reciprocal(out=inverse[:], in_=totals[step][:])
+            inverses[step] = inverse
+
         def normalise(step):
             tile_index, g = divmod(step, KV_HEADS)
             if g == 0:
                 rows = work.tile([P, FEATURES], BF16, tag="a", bufs=2)
                 a_rows[tile_index] = rows
-            total = small.tile([P, GROUP], F32, tag="total")
-            nc.vector.tensor_reduce(out=total[:], in_=row_sums[step][:], axis=ALONG_ROW, op=ALU.add)
-            inverse = small.tile([P, GROUP], F32, tag="inverse")
-            nc.vector.reciprocal(out=inverse[:], in_=total[:])
             nc.vector.tensor_tensor(
                 out=a_rows[tile_index][:, g * GROUP * HEAD_DIM : (g + 1) * GROUP * HEAD_DIM].rearrange(
                     "q (w j i) -> q j w i", w=2, j=GROUP
                 ),
                 in0=o_banks[step][:].rearrange("q j (i w) -> q j w i", w=2),
-                in1=inverse[:].unsqueeze(2).unsqueeze(3).broadcast_to([P, GROUP, 2, HEAD_DIM // 2]),
+                in1=inverses[step][:].unsqueeze(2).unsqueeze(3).broadcast_to([P, GROUP, 2, HEAD_DIM // 2]),
                 op=ALU.mult,
             )
 
@@ -321,7 +331,13 @@ def tile_qwen2dymemdecoderlayer_pa_kernel(tc, q_pos, k_mem, v_mem, Wo, out):
                 transpose_e(tick - TRANSPOSE_LAG)
             if 0 <= tick - QUANTISE_LAG < HEAD_TILES:
                 quantise_e(tick - QUANTISE_LAG)
+            if tick < HEAD_TILES:
+                find_shift(tick)
             step, rest = divmod(tick - VALUES_LAG, GROUP)
+            if rest == 0 and 0 <= step + 1 < STEPS:
+                add_row_sums(step + 1)
+            if rest == 1 and 0 <= step + 1 < STEPS:
+                invert_row_sums(step + 1)
             if rest == 0 and 0 <= step < STEPS:
                 weigh_values(step)
                 normalise(step)

@@ -37,6 +37,7 @@ OUT_COLS = 512
 OUT_BLOCKS = MODEL // OUT_COLS
 WO_ROWS = 2 * P
 WO_UNITS = (MODEL // WO_ROWS) * FEATURE_PASSES
+QUERY_UNITS = QUERY_TILES * (HEADS // BLOCKS)
 
 STEPS = ROW_TILES * KV_HEADS
 HEAD_TILES = STEPS * GROUP
@@ -49,8 +50,7 @@ A_PERIOD = A_STEPS * GROUP
 A_LAG = VALUES_LAG + (A_STEPS - 1) * GROUP + 2
 PROJECT_LAG = A_LAG + (QUERY_TILES * FEATURE_PASSES - 1) * A_PERIOD + 2
 WO_LAG = 4
-VECTOR_SHARE = 8
-SECOND_QUERIES_TICK = 4
+VECTOR_SHARE = 4
 LAST_TICK = A_LAG + (ROW_TILES * FEATURE_PASSES - 1) * A_PERIOD + 1
 
 FLOPS = 2 * (2 * BATCH * HEADS * QUERIES * SLOTS * HEAD_DIM) + 2 * BATCH * QUERIES * FEATURES * MODEL
@@ -98,18 +98,22 @@ def tile_qwen2dymemdecoderlayer_pa_kernel(tc, q_pos, k_mem, v_mem, Wo, out):
             copy(out=grouped[:], in_=bank[:].rearrange("p (c t) r -> p c r t", t=PACK))
             return grouped[:].rearrange("p c r t -> p (c r t)")
 
-        def load_queries(query_tile):
-            rows = loads.tile([P, HEADS * HEAD_DIM], BF16, tag="q_rows", bufs=2)
+        def load_queries(unit):
+            query_tile, half = divmod(unit, HEADS // BLOCKS)
+            rows = loads.tile([P, BLOCKS * HEAD_DIM], BF16, tag="q_rows", bufs=QUERY_UNITS)
             nc.sync.dma_start(
-                out=rows[:], in_=q_pos[query_tile * P : (query_tile + 1) * P].rearrange("q h d -> q (h d)")
+                out=rows[:],
+                in_=q_pos[query_tile * P : (query_tile + 1) * P, half * BLOCKS : (half + 1) * BLOCKS, :].rearrange(
+                    "q h d -> q (h d)"
+                ),
             )
-            q_rows[query_tile] = rows
+            q_rows[unit] = rows
 
-        def transpose_queries(query_tile):
-            for half in range(HEADS // BLOCKS):
-                bank = psum_misc.tile([P, BLOCKS, P], BF16, tag="misc")
-                transpose_blocks(bank, q_rows[query_tile][:, half * BLOCKS * P : (half + 1) * BLOCKS * P])
-                nc.vector.tensor_copy(out=q_t[:, query_tile, half * BLOCKS : (half + 1) * BLOCKS, :], in_=bank[:])
+        def transpose_queries(unit):
+            query_tile, half = divmod(unit, HEADS // BLOCKS)
+            bank = psum_misc.tile([P, BLOCKS, P], BF16, tag="misc")
+            transpose_blocks(bank, q_rows[unit])
+            nc.vector.tensor_copy(out=q_t[:, query_tile, half * BLOCKS : (half + 1) * BLOCKS, :], in_=bank[:])
 
         def load_keys(kv):
             b, g = divmod(kv, KV_HEADS)
@@ -290,12 +294,10 @@ def tile_qwen2dymemdecoderlayer_pa_kernel(tc, q_pos, k_mem, v_mem, Wo, out):
             cols = slice(c * P, (c + 1) * P)
             quantise(a_codes[:, tile_index, cols], a_scales[:, tile_index, cols], a_grouped[pass_index])
 
-        def project(block_index):
+        def project_passes(acc, block_index, passes):
             tile_index, block = divmod(block_index, OUT_BLOCKS)
-            b, query_tile = divmod(tile_index, QUERY_TILES)
             cols = slice(block * OUT_COLS, (block + 1) * OUT_COLS)
-            acc = psum_misc.tile([P, OUT_COLS], F32, tag="misc")
-            for c in range(FEATURE_PASSES):
+            for c in passes:
                 nc.tensor.matmul_mx(
                     out=acc[:],
                     lhsT=a_codes[:, tile_index, c * P : (c + 1) * P].bitcast(FP8X4),
@@ -305,23 +307,36 @@ def tile_qwen2dymemdecoderlayer_pa_kernel(tc, q_pos, k_mem, v_mem, Wo, out):
                     start=(c == 0),
                     stop=(c == FEATURE_PASSES - 1),
                 )
-            result = work.tile([P, OUT_COLS], F32, tag="result")
+
+        def store_block(acc, block_index):
+            tile_index, block = divmod(block_index, OUT_BLOCKS)
+            b, query_tile = divmod(tile_index, QUERY_TILES)
+            cols = slice(block * OUT_COLS, (block + 1) * OUT_COLS)
+            result = work.tile([P, OUT_COLS], F32, tag="result", bufs=OUT_BLOCKS)
             copy = nc.vector.tensor_copy if block % 2 == 0 else nc.scalar.copy
             copy(out=result[:], in_=acc[:])
             nc.sync.dma_start(out=out[b, query_tile * P : (query_tile + 1) * P, cols], in_=result[:])
+
+        def project(block_index):
+            acc = psum_misc.tile([P, OUT_COLS], F32, tag="misc")
+            project_passes(acc, block_index, range(FEATURE_PASSES))
+            store_block(acc, block_index)
 
         load_keys(0)
         load_queries(0)
         load_keys(1)
         load_values(0)
+        for unit in range(1, QUERY_UNITS):
+            load_queries(unit)
         load_keys(2)
         load_values(1)
-        load_queries(1)
         for pair in (0, 1):
             load_wo(pair)
         transpose_keys(0)
         transpose_queries(0)
 
+        last_blocks = range((ROW_TILES - 1) * OUT_BLOCKS, ROW_TILES * OUT_BLOCKS)
+        last_acc = {}
         for tick in range(LAST_TICK + 1):
             if tick < HEAD_TILES:
                 scores(tick)
@@ -341,6 +356,12 @@ def tile_qwen2dymemdecoderlayer_pa_kernel(tc, q_pos, k_mem, v_mem, Wo, out):
             if rest == 0 and 0 <= step < STEPS:
                 weigh_values(step)
                 normalise(step)
+            early = tick - TRANSPOSE_LAG - (HEAD_TILES - 2)
+            if 0 <= early < 2:
+                for block_index in last_blocks[2 * early : 2 * early + 2]:
+                    acc = psum_scores.tile([P, OUT_COLS], F32, tag="s")
+                    project_passes(acc, block_index, range(FEATURE_PASSES // 2))
+                    last_acc[block_index] = acc
             block_index, rest = divmod(tick - PROJECT_LAG, 2)
             if rest == 0 and 0 <= block_index < (ROW_TILES - 1) * OUT_BLOCKS:
                 project(block_index)
@@ -367,8 +388,9 @@ def tile_qwen2dymemdecoderlayer_pa_kernel(tc, q_pos, k_mem, v_mem, Wo, out):
                     load_values(kv + 2)
             if rest == 0 and 0 <= kv - 1 < KV:
                 quantise_values(kv - 1)
-            if tick == SECOND_QUERIES_TICK:
-                transpose_queries(1)
+            if 1 <= tick < QUERY_UNITS:
+                transpose_queries(tick)
 
-        for block in range(OUT_BLOCKS):
-            project((ROW_TILES - 1) * OUT_BLOCKS + block)
+        for block_index in last_blocks:
+            project_passes(last_acc[block_index], block_index, range(FEATURE_PASSES // 2, FEATURE_PASSES))
+            store_block(last_acc[block_index], block_index)

@@ -33,14 +33,17 @@ KV = BATCH * KV_HEADS
 SLOT_PASSES = SLOTS // K_PASS
 FEATURE_PASSES = FEATURES // K_PASS
 BLOCKS = 2 * PACK
-OUT_COLS = 512
-OUT_BLOCKS = MODEL // OUT_COLS
+Q_UNITS = QUERY_TILES * (HEADS // BLOCKS)
 WO_ROWS = 2 * P
-WO_UNITS = (MODEL // WO_ROWS) * FEATURE_PASSES
-QUERY_UNITS = QUERY_TILES * (HEADS // BLOCKS)
+WO_PAIRS = MODEL // WO_ROWS
+WO_UNITS = WO_PAIRS * FEATURE_PASSES
+PANEL = 512
+PANELS = MODEL // PANEL
 
 STEPS = ROW_TILES * KV_HEADS
 HEAD_TILES = STEPS * GROUP
+LOAD_AHEAD = 2
+
 EXP_LAG = 1
 TRANSPOSE_LAG = 2
 QUANTISE_LAG = 3
@@ -50,8 +53,8 @@ A_PERIOD = A_STEPS * GROUP
 A_LAG = VALUES_LAG + (A_STEPS - 1) * GROUP + 2
 PROJECT_LAG = A_LAG + (QUERY_TILES * FEATURE_PASSES - 1) * A_PERIOD + 2
 WO_LAG = 4
-VECTOR_SHARE = 4
 LAST_TICK = A_LAG + (ROW_TILES * FEATURE_PASSES - 1) * A_PERIOD + 1
+VECTOR_SHARE = 4
 
 FLOPS = 2 * (2 * BATCH * HEADS * QUERIES * SLOTS * HEAD_DIM) + 2 * BATCH * QUERIES * FEATURES * MODEL
 
@@ -60,12 +63,12 @@ def tile_qwen2dymemdecoderlayer_pa_kernel(tc, q_pos, k_mem, v_mem, Wo, out):
     nc = tc.nc
     with ExitStack() as ctx:
         keep = ctx.enter_context(tc.tile_pool(name="keep", bufs=1))
-        loads = ctx.enter_context(tc.tile_pool(name="loads", bufs=3))
+        loads = ctx.enter_context(tc.tile_pool(name="loads", bufs=LOAD_AHEAD + 1))
         work = ctx.enter_context(tc.tile_pool(name="work", bufs=3))
-        codes_pool = ctx.enter_context(tc.tile_pool(name="codes", bufs=6))
-        small = ctx.enter_context(tc.tile_pool(name="small", bufs=6))
-        psum_scores = ctx.enter_context(tc.psum_pool(name="psum_scores", bufs=4))
-        psum_et = ctx.enter_context(tc.psum_pool(name="psum_et", bufs=2))
+        codes_pool = ctx.enter_context(tc.tile_pool(name="codes", bufs=VALUES_LAG + 1))
+        small = ctx.enter_context(tc.tile_pool(name="small", bufs=VALUES_LAG + 1))
+        psum_scores = ctx.enter_context(tc.psum_pool(name="psum_scores", bufs=2 * SLOT_PASSES))
+        psum_blocks = ctx.enter_context(tc.psum_pool(name="psum_blocks", bufs=2))
         psum_misc = ctx.enter_context(tc.psum_pool(name="psum_misc", bufs=2))
         ctx.enter_context(tc.manual_schedule())
 
@@ -84,8 +87,9 @@ def tile_qwen2dymemdecoderlayer_pa_kernel(tc, q_pos, k_mem, v_mem, Wo, out):
         a_scales = keep.tile([P, ROW_TILES, FEATURE_PASSES * P], U8, align_bytes=64)
 
         q_rows, k_rows, v_rows, v_grouped, wo_rows, wo_grouped = {}, {}, {}, {}, {}, {}
-        score_banks, bank_tops, shifts, totals, inverses, row_sums, e_rows, e_grouped, e_mx, o_banks = {}, {}, {}, {}, {}, {}, {}, {}, {}, {}
-        a_rows, a_grouped = {}, {}
+        score_banks, bank_tops, shifts, e_rows, e_grouped, e_mx = {}, {}, {}, {}, {}, {}
+        row_sums, totals, inverses, o_banks = {}, {}, {}, {}
+        a_rows, a_grouped, last_acc = {}, {}, {}
 
         def quantise(codes, scales, grouped):
             nc.vector.quantize_mx(out=codes.bitcast(FP8X4), scales=scales, in_=grouped)
@@ -98,21 +102,21 @@ def tile_qwen2dymemdecoderlayer_pa_kernel(tc, q_pos, k_mem, v_mem, Wo, out):
             copy(out=grouped[:], in_=bank[:].rearrange("p (c t) r -> p c r t", t=PACK))
             return grouped[:].rearrange("p c r t -> p (c r t)")
 
-        def load_queries(unit):
-            query_tile, half = divmod(unit, HEADS // BLOCKS)
-            rows = loads.tile([P, BLOCKS * HEAD_DIM], BF16, tag="q_rows", bufs=QUERY_UNITS)
+        def load_queries(q_unit):
+            query_tile, half = divmod(q_unit, HEADS // BLOCKS)
+            rows = loads.tile([P, BLOCKS * HEAD_DIM], BF16, tag="q_rows", bufs=Q_UNITS)
             nc.sync.dma_start(
                 out=rows[:],
                 in_=q_pos[query_tile * P : (query_tile + 1) * P, half * BLOCKS : (half + 1) * BLOCKS, :].rearrange(
                     "q h d -> q (h d)"
                 ),
             )
-            q_rows[unit] = rows
+            q_rows[q_unit] = rows
 
-        def transpose_queries(unit):
-            query_tile, half = divmod(unit, HEADS // BLOCKS)
+        def transpose_queries(q_unit):
+            query_tile, half = divmod(q_unit, HEADS // BLOCKS)
             bank = psum_misc.tile([P, BLOCKS, P], BF16, tag="misc")
-            transpose_blocks(bank, q_rows[unit])
+            transpose_blocks(bank, q_rows[q_unit])
             nc.vector.tensor_copy(out=q_t[:, query_tile, half * BLOCKS : (half + 1) * BLOCKS, :], in_=bank[:])
 
         def load_keys(kv):
@@ -136,7 +140,7 @@ def tile_qwen2dymemdecoderlayer_pa_kernel(tc, q_pos, k_mem, v_mem, Wo, out):
             v_rows[kv] = rows
 
         def transpose_keys(kv):
-            bank = psum_et.tile([P, BLOCKS, P], BF16, tag="et")
+            bank = psum_blocks.tile([P, BLOCKS, P], BF16, tag="blocks")
             transpose_blocks(bank, k_rows[kv])
             nc.scalar.copy(out=k_t[:, kv, :], in_=bank[:].rearrange("p x m -> p (x m)"))
 
@@ -151,19 +155,19 @@ def tile_qwen2dymemdecoderlayer_pa_kernel(tc, q_pos, k_mem, v_mem, Wo, out):
         def load_wo(pair):
             rows = loads.tile([P, 2, FEATURES], BF16, tag="wo_rows")
             nc.sync.dma_start(
-                out=rows[:], in_=Wo[pair * WO_ROWS : (pair + 1) * WO_ROWS, :].rearrange("(x p) a -> p x a", p=P)
+                out=rows[:], in_=Wo[pair * WO_ROWS : (pair + 1) * WO_ROWS, :].rearrange("(y p) a -> p y a", p=P)
             )
             wo_rows[pair] = rows
 
-        def transpose_wo(unit):
-            pair, c = divmod(unit, FEATURE_PASSES)
+        def transpose_wo(wo_unit):
+            pair, c = divmod(wo_unit, FEATURE_PASSES)
             bank = psum_misc.tile([P, 2, WO_ROWS], F32, tag="misc")
             for u in range(2):
                 first = (2 * c + u) * P
-                for x in range(2):
+                for y in range(2):
                     nc.tensor.transpose(
-                        out=bank[:, u, x * P : (x + 1) * P],
-                        in_=wo_rows[pair][:, x, :].bitcast(F32)[:, first : first + P],
+                        out=bank[:, u, y * P : (y + 1) * P],
+                        in_=wo_rows[pair][:, y, :].bitcast(F32)[:, first : first + P],
                         identity=ident_f32[:],
                     )
             grouped = work.tile([P, WO_ROWS * PACK], BF16, tag="wo_grouped", align_bytes=64)
@@ -172,28 +176,27 @@ def tile_qwen2dymemdecoderlayer_pa_kernel(tc, q_pos, k_mem, v_mem, Wo, out):
                 out=grouped[:].bitcast(F32).rearrange("p (r u) -> p r u", u=2),
                 in_=bank[:].rearrange("p u r -> p r u"),
             )
-            wo_grouped[unit] = grouped
+            wo_grouped[wo_unit] = grouped
 
-        def quantise_wo(unit):
-            pair, c = divmod(unit, FEATURE_PASSES)
-            rows = slice(pair * WO_ROWS, (pair + 1) * WO_ROWS)
-            quantise(wo_codes[:, c, rows], wo_scales[:, c, rows], wo_grouped[unit][:])
+        def quantise_wo(wo_unit):
+            pair, c = divmod(wo_unit, FEATURE_PASSES)
+            cols = slice(pair * WO_ROWS, (pair + 1) * WO_ROWS)
+            quantise(wo_codes[:, c, cols], wo_scales[:, c, cols], wo_grouped[wo_unit][:])
 
         def place(i):
             step, j = divmod(i, GROUP)
-            tile_index, g = divmod(step, KV_HEADS)
-            return step, j, tile_index, (tile_index // QUERY_TILES) * KV_HEADS + g, g
-
+            row_tile, g = divmod(step, KV_HEADS)
+            return step, j, row_tile, (row_tile // QUERY_TILES) * KV_HEADS + g, g
 
         def scores(i):
-            step, j, tile_index, kv, g = place(i)
+            step, j, row_tile, kv, g = place(i)
             score_banks[i] = []
             tops = small.tile([P, SLOT_PASSES], F32, tag="tops")
             for c in range(SLOT_PASSES):
                 s = psum_scores.tile([P, K_PASS], F32, tag="s")
                 nc.tensor.matmul(
                     out=s[:],
-                    lhsT=q_t[:, tile_index % QUERY_TILES, GROUP * g + j, :],
+                    lhsT=q_t[:, row_tile % QUERY_TILES, GROUP * g + j, :],
                     rhs=k_t[:, kv, c * K_PASS : (c + 1) * K_PASS],
                     start=True,
                     stop=True,
@@ -211,7 +214,7 @@ def tile_qwen2dymemdecoderlayer_pa_kernel(tc, q_pos, k_mem, v_mem, Wo, out):
             shifts[i] = shift
 
         def exponentials(i):
-            step, j, tile_index, kv, g = place(i)
+            step, j, row_tile, kv, g = place(i)
             if j == 0:
                 sums = small.tile([P, GROUP, SLOT_PASSES], F32, tag="sums")
                 row_sums[step] = sums
@@ -228,7 +231,7 @@ def tile_qwen2dymemdecoderlayer_pa_kernel(tc, q_pos, k_mem, v_mem, Wo, out):
             e_rows[i] = e
 
         def transpose_e(i):
-            bank = psum_et.tile([P, BLOCKS, P], BF16, tag="et")
+            bank = psum_blocks.tile([P, BLOCKS, P], BF16, tag="blocks")
             transpose_blocks(bank, e_rows[i])
             grouped = work.tile([P, SLOT_PASSES, P, PACK], BF16, tag="e_grouped", align_bytes=64)
             to_vector = i >= HEAD_TILES // BATCH and i % VECTOR_SHARE == VECTOR_SHARE - 1
@@ -269,74 +272,74 @@ def tile_qwen2dymemdecoderlayer_pa_kernel(tc, q_pos, k_mem, v_mem, Wo, out):
             inverses[step] = inverse
 
         def normalise(step):
-            tile_index, g = divmod(step, KV_HEADS)
+            row_tile, g = divmod(step, KV_HEADS)
             if g == 0:
-                rows = work.tile([P, FEATURES], BF16, tag="a", bufs=2)
-                a_rows[tile_index] = rows
+                a = work.tile([P, FEATURES], BF16, tag="a", bufs=2)
+                a_rows[row_tile] = a
             nc.vector.tensor_tensor(
-                out=a_rows[tile_index][:, g * GROUP * HEAD_DIM : (g + 1) * GROUP * HEAD_DIM].rearrange(
-                    "q (w j i) -> q j w i", w=2, j=GROUP
+                out=a_rows[row_tile][:, g * GROUP * HEAD_DIM : (g + 1) * GROUP * HEAD_DIM].rearrange(
+                    "q (w j m) -> q j w m", w=2, j=GROUP
                 ),
-                in0=o_banks[step][:].rearrange("q j (i w) -> q j w i", w=2),
+                in0=o_banks[step][:].rearrange("q j (m w) -> q j w m", w=2),
                 in1=inverses[step][:].unsqueeze(2).unsqueeze(3).broadcast_to([P, GROUP, 2, HEAD_DIM // 2]),
                 op=ALU.mult,
             )
 
-        def transpose_a(pass_index):
-            tile_index, c = divmod(pass_index, FEATURE_PASSES)
-            bank = psum_et.tile([P, PACK, P], BF16, tag="et")
-            transpose_blocks(bank, a_rows[tile_index][:, c * K_PASS : (c + 1) * K_PASS])
+        def transpose_a(a_pass):
+            row_tile, c = divmod(a_pass, FEATURE_PASSES)
+            bank = psum_blocks.tile([P, PACK, P], BF16, tag="blocks")
+            transpose_blocks(bank, a_rows[row_tile][:, c * K_PASS : (c + 1) * K_PASS])
             grouped = work.tile([P, 1, P, PACK], BF16, tag="a_grouped", align_bytes=64)
-            a_grouped[pass_index] = group_words(nc.vector.tensor_copy, bank, grouped)
+            a_grouped[a_pass] = group_words(nc.vector.tensor_copy, bank, grouped)
 
-        def quantise_a(pass_index):
-            tile_index, c = divmod(pass_index, FEATURE_PASSES)
+        def quantise_a(a_pass):
+            row_tile, c = divmod(a_pass, FEATURE_PASSES)
             cols = slice(c * P, (c + 1) * P)
-            quantise(a_codes[:, tile_index, cols], a_scales[:, tile_index, cols], a_grouped[pass_index])
+            quantise(a_codes[:, row_tile, cols], a_scales[:, row_tile, cols], a_grouped[a_pass])
 
-        def project_passes(acc, block_index, passes):
-            tile_index, block = divmod(block_index, OUT_BLOCKS)
-            cols = slice(block * OUT_COLS, (block + 1) * OUT_COLS)
+        def project_passes(acc, panel, passes):
+            row_tile, n = divmod(panel, PANELS)
+            cols = slice(n * PANEL, (n + 1) * PANEL)
             for c in passes:
                 nc.tensor.matmul_mx(
                     out=acc[:],
-                    lhsT=a_codes[:, tile_index, c * P : (c + 1) * P].bitcast(FP8X4),
-                    lhsT_scale=a_scales[:, tile_index, c * P : (c + 1) * P],
+                    lhsT=a_codes[:, row_tile, c * P : (c + 1) * P].bitcast(FP8X4),
+                    lhsT_scale=a_scales[:, row_tile, c * P : (c + 1) * P],
                     rhs=wo_codes[:, c, cols].bitcast(FP8X4),
                     rhs_scale=wo_scales[:, c, cols],
                     start=(c == 0),
                     stop=(c == FEATURE_PASSES - 1),
                 )
 
-        def store_block(acc, block_index):
-            tile_index, block = divmod(block_index, OUT_BLOCKS)
-            b, query_tile = divmod(tile_index, QUERY_TILES)
-            cols = slice(block * OUT_COLS, (block + 1) * OUT_COLS)
-            result = work.tile([P, OUT_COLS], F32, tag="result", bufs=OUT_BLOCKS)
-            copy = nc.vector.tensor_copy if block % 2 == 0 else nc.scalar.copy
+        def store_panel(acc, panel):
+            row_tile, n = divmod(panel, PANELS)
+            b, query_tile = divmod(row_tile, QUERY_TILES)
+            result = work.tile([P, PANEL], F32, tag="result", bufs=PANELS)
+            copy = nc.vector.tensor_copy if n % 2 == 0 else nc.scalar.copy
             copy(out=result[:], in_=acc[:])
-            nc.sync.dma_start(out=out[b, query_tile * P : (query_tile + 1) * P, cols], in_=result[:])
+            nc.sync.dma_start(
+                out=out[b, query_tile * P : (query_tile + 1) * P, n * PANEL : (n + 1) * PANEL], in_=result[:]
+            )
 
-        def project(block_index):
-            acc = psum_misc.tile([P, OUT_COLS], F32, tag="misc")
-            project_passes(acc, block_index, range(FEATURE_PASSES))
-            store_block(acc, block_index)
+        def project(panel):
+            acc = psum_misc.tile([P, PANEL], F32, tag="misc")
+            project_passes(acc, panel, range(FEATURE_PASSES))
+            store_panel(acc, panel)
 
         load_keys(0)
         load_queries(0)
         load_keys(1)
         load_values(0)
-        for unit in range(1, QUERY_UNITS):
-            load_queries(unit)
+        for q_unit in range(1, Q_UNITS):
+            load_queries(q_unit)
         load_keys(2)
         load_values(1)
-        for pair in (0, 1):
+        for pair in range(LOAD_AHEAD):
             load_wo(pair)
         transpose_keys(0)
         transpose_queries(0)
 
-        last_blocks = range((ROW_TILES - 1) * OUT_BLOCKS, ROW_TILES * OUT_BLOCKS)
-        last_acc = {}
+        last_panels = range((ROW_TILES - 1) * PANELS, ROW_TILES * PANELS)
         for tick in range(LAST_TICK + 1):
             if tick < HEAD_TILES:
                 scores(tick)
@@ -348,6 +351,7 @@ def tile_qwen2dymemdecoderlayer_pa_kernel(tc, q_pos, k_mem, v_mem, Wo, out):
                 quantise_e(tick - QUANTISE_LAG)
             if tick < HEAD_TILES:
                 find_shift(tick)
+
             step, rest = divmod(tick - VALUES_LAG, GROUP)
             if rest == 0 and 0 <= step + 1 < STEPS:
                 add_row_sums(step + 1)
@@ -356,41 +360,46 @@ def tile_qwen2dymemdecoderlayer_pa_kernel(tc, q_pos, k_mem, v_mem, Wo, out):
             if rest == 0 and 0 <= step < STEPS:
                 weigh_values(step)
                 normalise(step)
+
             early = tick - TRANSPOSE_LAG - (HEAD_TILES - 2)
             if 0 <= early < 2:
-                for block_index in last_blocks[2 * early : 2 * early + 2]:
-                    acc = psum_scores.tile([P, OUT_COLS], F32, tag="s")
-                    project_passes(acc, block_index, range(FEATURE_PASSES // 2))
-                    last_acc[block_index] = acc
-            block_index, rest = divmod(tick - PROJECT_LAG, 2)
-            if rest == 0 and 0 <= block_index < (ROW_TILES - 1) * OUT_BLOCKS:
-                project(block_index)
-            pass_index, rest = divmod(tick - A_LAG, A_PERIOD)
-            if rest == 0 and pass_index >= 0:
-                transpose_a(pass_index)
-            if rest == 1 and pass_index >= 0:
-                quantise_a(pass_index)
+                for panel in last_panels[2 * early : 2 * early + 2]:
+                    acc = psum_scores.tile([P, PANEL], F32, tag="s")
+                    project_passes(acc, panel, range(FEATURE_PASSES // 2))
+                    last_acc[panel] = acc
+            panel, rest = divmod(tick - PROJECT_LAG, 2)
+            if rest == 0 and 0 <= panel < last_panels[0]:
+                project(panel)
+
+            a_pass, rest = divmod(tick - A_LAG, A_PERIOD)
+            if rest == 0 and a_pass >= 0:
+                transpose_a(a_pass)
+            if rest == 1 and a_pass >= 0:
+                quantise_a(a_pass)
+
             if 0 <= tick - WO_LAG - 1 < WO_UNITS:
                 quantise_wo(tick - WO_LAG - 1)
             if 0 <= tick - WO_LAG < WO_UNITS:
                 transpose_wo(tick - WO_LAG)
                 pair, c = divmod(tick - WO_LAG, FEATURE_PASSES)
-                if c == 0 and pair + 2 < MODEL // WO_ROWS:
-                    load_wo(pair + 2)
+                if c == 0 and pair + LOAD_AHEAD < WO_PAIRS:
+                    load_wo(pair + LOAD_AHEAD)
+
             kv, rest = divmod(tick, 2)
             if rest == 0 and kv + 1 < KV:
                 transpose_keys(kv + 1)
-                if kv + 3 < KV:
-                    load_keys(kv + 3)
+                if kv + 1 + LOAD_AHEAD < KV:
+                    load_keys(kv + 1 + LOAD_AHEAD)
             if rest == 1 and kv < KV:
                 group_values(kv)
-                if kv + 2 < KV:
-                    load_values(kv + 2)
+                if kv + LOAD_AHEAD < KV:
+                    load_values(kv + LOAD_AHEAD)
             if rest == 0 and 0 <= kv - 1 < KV:
                 quantise_values(kv - 1)
-            if 1 <= tick < QUERY_UNITS:
+
+            if 1 <= tick < Q_UNITS:
                 transpose_queries(tick)
 
-        for block_index in last_blocks:
-            project_passes(last_acc[block_index], block_index, range(FEATURE_PASSES // 2, FEATURE_PASSES))
-            store_block(last_acc[block_index], block_index)
+        for panel in last_panels:
+            project_passes(last_acc[panel], panel, range(FEATURE_PASSES // 2, FEATURE_PASSES))
+            store_panel(last_acc[panel], panel)

@@ -99,8 +99,17 @@ def tile_qwen2dymemdecoderlayer_pa_kernel(tc, q_pos, k_mem, v_mem, Wo, out):
                 nc.tensor.transpose(out=bank[:, x, :], in_=rows[:, x * P : (x + 1) * P], identity=ident_bf16[:])
 
         def group_words(copy, bank, grouped):
-            copy(out=grouped[:], in_=bank[:].rearrange("p (c t) r -> p c r t", t=PACK))
-            return grouped[:].rearrange("p c r t -> p (c r t)")
+            flat = grouped[:].rearrange("p c r t -> p (c r t)")
+            copy(
+                out=flat.bitcast(F32).rearrange("p (c r u) -> p c r u", r=P, u=2),
+                in_=bank[:].rearrange("p (c u) r -> p c r u", u=2),
+            )
+            return flat
+
+        def transpose_words(bank, rows):
+            words = rows.bitcast(F32)
+            for x in range(words.shape[1] // P):
+                nc.tensor.transpose(out=bank[:, x, :], in_=words[:, x * P : (x + 1) * P], identity=ident_f32[:])
 
         def load_queries(q_unit):
             query_tile, half = divmod(q_unit, HEADS // BLOCKS)
@@ -221,8 +230,8 @@ def tile_qwen2dymemdecoderlayer_pa_kernel(tc, q_pos, k_mem, v_mem, Wo, out):
             e = work.tile([P, SLOTS], BF16, tag="e")
             for c in range(SLOT_PASSES):
                 nc.scalar.activation(
-                    out=e[:, c * K_PASS : (c + 1) * K_PASS],
-                    in_=score_banks[i][c][:],
+                    out=e[:, c * K_PASS : (c + 1) * K_PASS].rearrange("q (u p w) -> q u p w", u=2, w=2),
+                    in_=score_banks[i][c][:].rearrange("q (u w p) -> q u p w", u=2, w=2),
                     func=EXP,
                     bias=shifts[i][:],
                     scale=SCORE_FACTOR,
@@ -231,8 +240,8 @@ def tile_qwen2dymemdecoderlayer_pa_kernel(tc, q_pos, k_mem, v_mem, Wo, out):
             e_rows[i] = e
 
         def transpose_e(i):
-            bank = psum_blocks.tile([P, BLOCKS, P], BF16, tag="blocks")
-            transpose_blocks(bank, e_rows[i])
+            bank = psum_blocks.tile([P, 2 * SLOT_PASSES, P], F32, tag="blocks")
+            transpose_words(bank, e_rows[i][:])
             grouped = work.tile([P, SLOT_PASSES, P, PACK], BF16, tag="e_grouped", align_bytes=64)
             to_vector = i >= HEAD_TILES // BATCH and i % VECTOR_SHARE == VECTOR_SHARE - 1
             e_grouped[i] = group_words(nc.vector.tensor_copy if to_vector else nc.scalar.copy, bank, grouped)
@@ -278,17 +287,17 @@ def tile_qwen2dymemdecoderlayer_pa_kernel(tc, q_pos, k_mem, v_mem, Wo, out):
                 a_rows[row_tile] = a
             nc.vector.tensor_tensor(
                 out=a_rows[row_tile][:, g * GROUP * HEAD_DIM : (g + 1) * GROUP * HEAD_DIM].rearrange(
-                    "q (w j m) -> q j w m", w=2, j=GROUP
+                    "q (j d) -> q j d", j=GROUP
                 ),
-                in0=o_banks[step][:].rearrange("q j (m w) -> q j w m", w=2),
-                in1=inverses[step][:].unsqueeze(2).unsqueeze(3).broadcast_to([P, GROUP, 2, HEAD_DIM // 2]),
+                in0=o_banks[step][:],
+                in1=inverses[step][:].unsqueeze(2).broadcast_to([P, GROUP, HEAD_DIM]),
                 op=ALU.mult,
             )
 
         def transpose_a(a_pass):
             row_tile, c = divmod(a_pass, FEATURE_PASSES)
-            bank = psum_blocks.tile([P, PACK, P], BF16, tag="blocks")
-            transpose_blocks(bank, a_rows[row_tile][:, c * K_PASS : (c + 1) * K_PASS])
+            bank = psum_blocks.tile([P, 2, P], F32, tag="blocks")
+            transpose_words(bank, a_rows[row_tile][:, c * K_PASS : (c + 1) * K_PASS])
             grouped = work.tile([P, 1, P, PACK], BF16, tag="a_grouped", align_bytes=64)
             a_grouped[a_pass] = group_words(nc.vector.tensor_copy, bank, grouped)
 

@@ -40,36 +40,43 @@ WO_UNITS = WO_PAIRS * FEATURE_PASSES
 PANEL = 512
 PANELS = MODEL // PANEL
 
-STEPS = ROW_TILES * KV_HEADS
-HEAD_TILES = STEPS * GROUP
+TILES = K_PASS // HEAD_DIM
+A_UNITS = ROW_TILES * FEATURE_PASSES
+HEAD_TILES = A_UNITS * TILES
 LOAD_AHEAD = 2
 
 EXP_LAG = 1
 TRANSPOSE_LAG = 2
 QUANTISE_LAG = 3
-VALUES_LAG = QUANTISE_LAG + GROUP
-A_STEPS = K_PASS // (GROUP * HEAD_DIM)
-A_PERIOD = A_STEPS * GROUP
-A_LAG = VALUES_LAG + (A_STEPS - 1) * GROUP + 2
-PROJECT_LAG = A_LAG + (QUERY_TILES * FEATURE_PASSES - 1) * A_PERIOD + 2
-WO_LAG = 4
-LAST_TICK = A_LAG + (ROW_TILES * FEATURE_PASSES - 1) * A_PERIOD + 1
-VECTOR_SHARE = 4
+SUM_LAG = EXP_LAG + 1
+INVERT_LAG = SUM_LAG + 1
+VALUES_LAG = QUANTISE_LAG + 1
+A_LAG = VALUES_LAG + 1
+PREP_PERIOD = 3
+WO_START = 5
+PROJECT_START = 42
+LAST_TICK = HEAD_TILES - 1 + A_LAG + 1
 
 FLOPS = 2 * (2 * BATCH * HEADS * QUERIES * SLOTS * HEAD_DIM) + 2 * BATCH * QUERIES * FEATURES * MODEL
 
 
+def a_unit_order():
+    first = [(query_tile, c) for c in range(FEATURE_PASSES) for query_tile in range(QUERY_TILES)]
+    second = [(QUERY_TILES + query_tile, c) for query_tile in range(QUERY_TILES) for c in range(FEATURE_PASSES)]
+    return first + second
+
+
 def tile_qwen2dymemdecoderlayer_pa_kernel(tc, q_pos, k_mem, v_mem, Wo, out):
     nc = tc.nc
+    a_order = a_unit_order()
     with ExitStack() as ctx:
         keep = ctx.enter_context(tc.tile_pool(name="keep", bufs=1))
         loads = ctx.enter_context(tc.tile_pool(name="loads", bufs=LOAD_AHEAD + 1))
         work = ctx.enter_context(tc.tile_pool(name="work", bufs=3))
-        codes_pool = ctx.enter_context(tc.tile_pool(name="codes", bufs=VALUES_LAG + 1))
-        small = ctx.enter_context(tc.tile_pool(name="small", bufs=VALUES_LAG + 1))
+        codes_pool = ctx.enter_context(tc.tile_pool(name="codes", bufs=TILES + VALUES_LAG))
+        small = ctx.enter_context(tc.tile_pool(name="small", bufs=4))
         psum_scores = ctx.enter_context(tc.psum_pool(name="psum_scores", bufs=2 * SLOT_PASSES))
-        psum_blocks = ctx.enter_context(tc.psum_pool(name="psum_blocks", bufs=2))
-        psum_misc = ctx.enter_context(tc.psum_pool(name="psum_misc", bufs=2))
+        psum_misc = ctx.enter_context(tc.psum_pool(name="psum_misc", bufs=4))
         ctx.enter_context(tc.manual_schedule())
 
         ident_bf16 = keep.tile([P, P], BF16)
@@ -88,8 +95,8 @@ def tile_qwen2dymemdecoderlayer_pa_kernel(tc, q_pos, k_mem, v_mem, Wo, out):
 
         q_rows, k_rows, v_rows, v_grouped, wo_rows, wo_grouped = {}, {}, {}, {}, {}, {}
         score_banks, bank_tops, shifts, e_rows, e_grouped, e_mx = {}, {}, {}, {}, {}, {}
-        row_sums, totals, inverses, o_banks = {}, {}, {}, {}
-        a_rows, a_grouped, last_acc = {}, {}, {}
+        row_sums, totals, inverses, a_rows, a_grouped = {}, {}, {}, {}, {}
+        panel_acc, last_acc = {}, {}
 
         def quantise(codes, scales, grouped):
             nc.vector.quantize_mx(out=codes.bitcast(FP8X4), scales=scales, in_=grouped)
@@ -97,6 +104,11 @@ def tile_qwen2dymemdecoderlayer_pa_kernel(tc, q_pos, k_mem, v_mem, Wo, out):
         def transpose_blocks(bank, rows):
             for x in range(rows.shape[1] // P):
                 nc.tensor.transpose(out=bank[:, x, :], in_=rows[:, x * P : (x + 1) * P], identity=ident_bf16[:])
+
+        def transpose_words(bank, rows):
+            words = rows.bitcast(F32)
+            for x in range(words.shape[1] // P):
+                nc.tensor.transpose(out=bank[:, x, :], in_=words[:, x * P : (x + 1) * P], identity=ident_f32[:])
 
         def group_words(copy, bank, grouped):
             flat = grouped[:].rearrange("p c r t -> p (c r t)")
@@ -106,13 +118,8 @@ def tile_qwen2dymemdecoderlayer_pa_kernel(tc, q_pos, k_mem, v_mem, Wo, out):
             )
             return flat
 
-        def transpose_words(bank, rows):
-            words = rows.bitcast(F32)
-            for x in range(words.shape[1] // P):
-                nc.tensor.transpose(out=bank[:, x, :], in_=words[:, x * P : (x + 1) * P], identity=ident_f32[:])
-
         def load_queries(q_unit):
-            query_tile, half = divmod(q_unit, HEADS // BLOCKS)
+            half, query_tile = divmod(q_unit, QUERY_TILES)
             rows = loads.tile([P, BLOCKS * HEAD_DIM], BF16, tag="q_rows", bufs=Q_UNITS)
             nc.sync.dma_start(
                 out=rows[:],
@@ -123,7 +130,7 @@ def tile_qwen2dymemdecoderlayer_pa_kernel(tc, q_pos, k_mem, v_mem, Wo, out):
             q_rows[q_unit] = rows
 
         def transpose_queries(q_unit):
-            query_tile, half = divmod(q_unit, HEADS // BLOCKS)
+            half, query_tile = divmod(q_unit, QUERY_TILES)
             bank = psum_misc.tile([P, BLOCKS, P], BF16, tag="misc")
             transpose_blocks(bank, q_rows[q_unit])
             nc.vector.tensor_copy(out=q_t[:, query_tile, half * BLOCKS : (half + 1) * BLOCKS, :], in_=bank[:])
@@ -149,14 +156,24 @@ def tile_qwen2dymemdecoderlayer_pa_kernel(tc, q_pos, k_mem, v_mem, Wo, out):
             v_rows[kv] = rows
 
         def transpose_keys(kv):
-            bank = psum_blocks.tile([P, BLOCKS, P], BF16, tag="blocks")
+            bank = psum_misc.tile([P, BLOCKS, P], BF16, tag="misc")
             transpose_blocks(bank, k_rows[kv])
-            nc.scalar.copy(out=k_t[:, kv, :], in_=bank[:].rearrange("p x m -> p (x m)"))
+            nc.vector.tensor_copy(out=k_t[:, kv, :], in_=bank[:].rearrange("p x m -> p (x m)"))
 
-        def group_values(kv):
-            grouped = work.tile([P, SLOT_PASSES, HEAD_DIM, PACK], BF16, tag="v_grouped", align_bytes=64)
-            nc.vector.tensor_copy(out=grouped[:], in_=v_rows[kv][:].rearrange("p c t d -> p c d t"))
-            v_grouped[kv] = grouped
+        def group_values(kv, piece):
+            if piece == 0:
+                grouped = work.tile([P, SLOT_PASSES, HEAD_DIM, PACK], BF16, tag="v_grouped", align_bytes=64)
+                v_grouped[kv] = grouped
+            c, half = divmod(piece, 2)
+            d = slice(half * (HEAD_DIM // 2), (half + 1) * (HEAD_DIM // 2))
+            nc.gpsimd.tensor_scalar(
+                out=v_grouped[kv][:, c, d, :],
+                in0=v_rows[kv][:, c, :, d].rearrange("p t d -> p d t"),
+                scalar1=1.0,
+                scalar2=0.0,
+                op0=ALU.mult,
+                op1=ALU.add,
+            )
 
         def quantise_values(kv):
             quantise(v_codes[:, kv, :], v_scales[:, kv, :], v_grouped[kv][:].rearrange("p c d t -> p (c d t)"))
@@ -180,8 +197,7 @@ def tile_qwen2dymemdecoderlayer_pa_kernel(tc, q_pos, k_mem, v_mem, Wo, out):
                         identity=ident_f32[:],
                     )
             grouped = work.tile([P, WO_ROWS * PACK], BF16, tag="wo_grouped", align_bytes=64)
-            copy = nc.scalar.copy if c % 2 == 0 else nc.vector.tensor_copy
-            copy(
+            nc.scalar.copy(
                 out=grouped[:].bitcast(F32).rearrange("p (r u) -> p r u", u=2),
                 in_=bank[:].rearrange("p u r -> p r u"),
             )
@@ -193,19 +209,20 @@ def tile_qwen2dymemdecoderlayer_pa_kernel(tc, q_pos, k_mem, v_mem, Wo, out):
             quantise(wo_codes[:, c, cols], wo_scales[:, c, cols], wo_grouped[wo_unit][:])
 
         def place(i):
-            step, j = divmod(i, GROUP)
-            row_tile, g = divmod(step, KV_HEADS)
-            return step, j, row_tile, (row_tile // QUERY_TILES) * KV_HEADS + g, g
+            unit, x = divmod(i, TILES)
+            row_tile, c = a_order[unit]
+            head = TILES * c + x
+            return unit, x, head, row_tile, (row_tile // QUERY_TILES) * KV_HEADS + head // GROUP
 
         def scores(i):
-            step, j, row_tile, kv, g = place(i)
+            unit, x, head, row_tile, kv = place(i)
             score_banks[i] = []
             tops = small.tile([P, SLOT_PASSES], F32, tag="tops")
             for c in range(SLOT_PASSES):
                 s = psum_scores.tile([P, K_PASS], F32, tag="s")
                 nc.tensor.matmul(
                     out=s[:],
-                    lhsT=q_t[:, row_tile % QUERY_TILES, GROUP * g + j, :],
+                    lhsT=q_t[:, row_tile % QUERY_TILES, head, :],
                     rhs=k_t[:, kv, c * K_PASS : (c + 1) * K_PASS],
                     start=True,
                     stop=True,
@@ -217,16 +234,16 @@ def tile_qwen2dymemdecoderlayer_pa_kernel(tc, q_pos, k_mem, v_mem, Wo, out):
         def find_shift(i):
             tops = bank_tops[i]
             shift = small.tile([P, 1], F32, tag="shift")
-            nc.vector.tensor_scalar(
+            nc.gpsimd.tensor_scalar(
                 out=shift[:], in0=tops[:, 0:1], scalar1=tops[:, 1:2], scalar2=-SCORE_FACTOR, op0=ALU.max, op1=ALU.mult
             )
             shifts[i] = shift
 
         def exponentials(i):
-            step, j, row_tile, kv, g = place(i)
-            if j == 0:
-                sums = small.tile([P, GROUP, SLOT_PASSES], F32, tag="sums")
-                row_sums[step] = sums
+            unit, x = divmod(i, TILES)
+            if x == 0:
+                sums = small.tile([P, TILES, SLOT_PASSES], F32, tag="sums")
+                row_sums[unit] = sums
             e = work.tile([P, SLOTS], BF16, tag="e")
             for c in range(SLOT_PASSES):
                 nc.scalar.activation(
@@ -235,16 +252,15 @@ def tile_qwen2dymemdecoderlayer_pa_kernel(tc, q_pos, k_mem, v_mem, Wo, out):
                     func=EXP,
                     bias=shifts[i][:],
                     scale=SCORE_FACTOR,
-                    accum_out=row_sums[step][:, j, c : c + 1],
+                    accum_out=row_sums[unit][:, x, c : c + 1],
                 )
             e_rows[i] = e
 
         def transpose_e(i):
-            bank = psum_blocks.tile([P, 2 * SLOT_PASSES, P], F32, tag="blocks")
+            bank = psum_misc.tile([P, 2 * SLOT_PASSES, P], F32, tag="misc")
             transpose_words(bank, e_rows[i][:])
             grouped = work.tile([P, SLOT_PASSES, P, PACK], BF16, tag="e_grouped", align_bytes=64)
-            to_vector = i >= HEAD_TILES // BATCH and i % VECTOR_SHARE == VECTOR_SHARE - 1
-            e_grouped[i] = group_words(nc.vector.tensor_copy if to_vector else nc.scalar.copy, bank, grouped)
+            e_grouped[i] = group_words(nc.scalar.copy, bank, grouped)
 
         def quantise_e(i):
             e_codes = codes_pool.tile([P, SLOT_PASSES * P], U32, tag="e_codes", align_bytes=64)
@@ -252,15 +268,26 @@ def tile_qwen2dymemdecoderlayer_pa_kernel(tc, q_pos, k_mem, v_mem, Wo, out):
             quantise(e_codes[:], e_scales[:], e_grouped[i])
             e_mx[i] = (e_codes, e_scales)
 
-        def weigh_values(step):
-            kv = place(GROUP * step)[3]
-            o = psum_misc.tile([P, GROUP, HEAD_DIM], F32, tag="misc")
-            for j in range(GROUP):
-                e_codes, e_scales = e_mx[GROUP * step + j]
+        def add_row_sums(unit):
+            total = small.tile([P, TILES], F32, tag="total")
+            sums = row_sums[unit]
+            nc.gpsimd.tensor_tensor(out=total[:], in0=sums[:, :, 0], in1=sums[:, :, 1], op=ALU.add)
+            totals[unit] = total
+
+        def invert_row_sums(unit):
+            inverse = small.tile([P, TILES], F32, tag="inverse")
+            nc.vector.reciprocal(out=inverse[:], in_=totals[unit][:])
+            inverses[unit] = inverse
+
+        def weigh_values(unit):
+            o = psum_misc.tile([P, TILES, HEAD_DIM], F32, tag="misc")
+            for i in range(unit * TILES, (unit + 1) * TILES):
+                kv = place(i)[4]
+                e_codes, e_scales = e_mx[i]
                 for c in range(SLOT_PASSES):
                     cols = slice(c * P, (c + 1) * P)
                     nc.tensor.matmul_mx(
-                        out=o[:, j, :],
+                        out=o[:, i % TILES, :],
                         lhsT=e_codes[:, cols].bitcast(FP8X4),
                         lhsT_scale=e_scales[:, cols],
                         rhs=v_codes[:, kv, cols].bitcast(FP8X4),
@@ -268,46 +295,27 @@ def tile_qwen2dymemdecoderlayer_pa_kernel(tc, q_pos, k_mem, v_mem, Wo, out):
                         start=(c == 0),
                         stop=(c == SLOT_PASSES - 1),
                     )
-            o_banks[step] = o
-
-        def add_row_sums(step):
-            total = small.tile([P, GROUP], F32, tag="total")
-            nc.vector.tensor_reduce(out=total[:], in_=row_sums[step][:], axis=ALONG_ROW, op=ALU.add)
-            totals[step] = total
-
-        def invert_row_sums(step):
-            inverse = small.tile([P, GROUP], F32, tag="inverse")
-            nc.vector.reciprocal(out=inverse[:], in_=totals[step][:])
-            inverses[step] = inverse
-
-        def normalise(step):
-            row_tile, g = divmod(step, KV_HEADS)
-            if g == 0:
-                a = work.tile([P, FEATURES], BF16, tag="a", bufs=2)
-                a_rows[row_tile] = a
+            a = work.tile([P, TILES, HEAD_DIM], BF16, tag="a")
             nc.vector.tensor_tensor(
-                out=a_rows[row_tile][:, g * GROUP * HEAD_DIM : (g + 1) * GROUP * HEAD_DIM].rearrange(
-                    "q (j d) -> q j d", j=GROUP
-                ),
-                in0=o_banks[step][:],
-                in1=inverses[step][:].unsqueeze(2).broadcast_to([P, GROUP, HEAD_DIM]),
+                out=a[:],
+                in0=o[:],
+                in1=inverses[unit][:].unsqueeze(2).broadcast_to([P, TILES, HEAD_DIM]),
                 op=ALU.mult,
             )
+            a_rows[unit] = a
 
-        def transpose_a(a_pass):
-            row_tile, c = divmod(a_pass, FEATURE_PASSES)
-            bank = psum_blocks.tile([P, 2, P], F32, tag="blocks")
-            transpose_words(bank, a_rows[row_tile][:, c * K_PASS : (c + 1) * K_PASS])
+        def transpose_a(unit):
+            bank = psum_misc.tile([P, 2, P], F32, tag="misc")
+            transpose_words(bank, a_rows[unit][:].rearrange("q x d -> q (x d)"))
             grouped = work.tile([P, 1, P, PACK], BF16, tag="a_grouped", align_bytes=64)
-            a_grouped[a_pass] = group_words(nc.vector.tensor_copy, bank, grouped)
+            a_grouped[unit] = group_words(nc.vector.tensor_copy, bank, grouped)
 
-        def quantise_a(a_pass):
-            row_tile, c = divmod(a_pass, FEATURE_PASSES)
+        def quantise_a(unit):
+            row_tile, c = a_order[unit]
             cols = slice(c * P, (c + 1) * P)
-            quantise(a_codes[:, row_tile, cols], a_scales[:, row_tile, cols], a_grouped[a_pass])
+            quantise(a_codes[:, row_tile, cols], a_scales[:, row_tile, cols], a_grouped[unit])
 
-        def project_passes(acc, panel, passes):
-            row_tile, n = divmod(panel, PANELS)
+        def project_passes(acc, row_tile, n, passes):
             cols = slice(n * PANEL, (n + 1) * PANEL)
             for c in passes:
                 nc.tensor.matmul_mx(
@@ -320,95 +328,116 @@ def tile_qwen2dymemdecoderlayer_pa_kernel(tc, q_pos, k_mem, v_mem, Wo, out):
                     stop=(c == FEATURE_PASSES - 1),
                 )
 
-        def store_panel(acc, panel):
-            row_tile, n = divmod(panel, PANELS)
+        def store_panel(acc, row_tile, n):
             b, query_tile = divmod(row_tile, QUERY_TILES)
             result = work.tile([P, PANEL], F32, tag="result", bufs=PANELS)
-            copy = nc.vector.tensor_copy if n % 2 == 0 else nc.scalar.copy
+            copy = nc.scalar.copy if n % 4 == 3 else nc.vector.tensor_copy
             copy(out=result[:], in_=acc[:])
             nc.sync.dma_start(
                 out=out[b, query_tile * P : (query_tile + 1) * P, n * PANEL : (n + 1) * PANEL], in_=result[:]
             )
 
-        def project(panel):
-            acc = psum_misc.tile([P, PANEL], F32, tag="misc")
-            project_passes(acc, panel, range(FEATURE_PASSES))
-            store_panel(acc, panel)
+        def project(row_tile, n, half):
+            if half == 0:
+                acc = psum_misc.tile([P, PANEL], F32, tag="misc")
+                panel_acc[row_tile, n] = acc
+            acc = panel_acc[row_tile, n]
+            project_passes(acc, row_tile, n, range(half * FEATURE_PASSES // 2, (half + 1) * FEATURE_PASSES // 2))
+            if half == 1:
+                store_panel(acc, row_tile, n)
 
         load_keys(0)
         load_queries(0)
         load_keys(1)
         load_values(0)
-        for q_unit in range(1, Q_UNITS):
-            load_queries(q_unit)
-        load_keys(2)
+        load_queries(1)
         load_values(1)
+        load_keys(2)
+        load_queries(2)
+        load_queries(3)
         for pair in range(LOAD_AHEAD):
             load_wo(pair)
         transpose_keys(0)
         transpose_queries(0)
 
-        last_panels = range((ROW_TILES - 1) * PANELS, ROW_TILES * PANELS)
+        panels = [(row_tile, n) for n in range(PANELS) for row_tile in range(QUERY_TILES)]
+        panels += [(row_tile, n) for row_tile in range(QUERY_TILES, ROW_TILES - 1) for n in range(PANELS)]
+        last_row_tile = ROW_TILES - 1
         for tick in range(LAST_TICK + 1):
             if tick < HEAD_TILES:
                 scores(tick)
-            if 0 <= tick - EXP_LAG < HEAD_TILES:
-                exponentials(tick - EXP_LAG)
-            if 0 <= tick - TRANSPOSE_LAG < HEAD_TILES:
-                transpose_e(tick - TRANSPOSE_LAG)
-            if 0 <= tick - QUANTISE_LAG < HEAD_TILES:
-                quantise_e(tick - QUANTISE_LAG)
-            if tick < HEAD_TILES:
                 find_shift(tick)
 
-            step, rest = divmod(tick - VALUES_LAG, GROUP)
-            if rest == 0 and 0 <= step + 1 < STEPS:
-                add_row_sums(step + 1)
-            if rest == 1 and 0 <= step + 1 < STEPS:
-                invert_row_sums(step + 1)
-            if rest == 0 and 0 <= step < STEPS:
-                weigh_values(step)
-                normalise(step)
+            if 0 <= tick - EXP_LAG < HEAD_TILES:
+                exponentials(tick - EXP_LAG)
 
-            early = tick - TRANSPOSE_LAG - (HEAD_TILES - 2)
-            if 0 <= early < 2:
-                for panel in last_panels[2 * early : 2 * early + 2]:
-                    acc = psum_scores.tile([P, PANEL], F32, tag="s")
-                    project_passes(acc, panel, range(FEATURE_PASSES // 2))
-                    last_acc[panel] = acc
-            panel, rest = divmod(tick - PROJECT_LAG, 2)
-            if rest == 0 and 0 <= panel < last_panels[0]:
-                project(panel)
+            if 0 <= tick - TRANSPOSE_LAG < HEAD_TILES:
+                transpose_e(tick - TRANSPOSE_LAG)
 
-            a_pass, rest = divmod(tick - A_LAG, A_PERIOD)
-            if rest == 0 and a_pass >= 0:
-                transpose_a(a_pass)
-            if rest == 1 and a_pass >= 0:
-                quantise_a(a_pass)
+            if 0 <= tick - QUANTISE_LAG < HEAD_TILES:
+                quantise_e(tick - QUANTISE_LAG)
 
-            if 0 <= tick - WO_LAG - 1 < WO_UNITS:
-                quantise_wo(tick - WO_LAG - 1)
-            if 0 <= tick - WO_LAG < WO_UNITS:
-                transpose_wo(tick - WO_LAG)
-                pair, c = divmod(tick - WO_LAG, FEATURE_PASSES)
+            unit, rest = divmod(tick - (TILES - 1) - SUM_LAG, TILES)
+            if rest == 0 and 0 <= unit < A_UNITS:
+                add_row_sums(unit)
+
+            unit, rest = divmod(tick - (TILES - 1) - INVERT_LAG, TILES)
+            if rest == 0 and 0 <= unit < A_UNITS:
+                invert_row_sums(unit)
+
+            round_, rest = divmod(tick - WO_START, PREP_PERIOD)
+            wo_unit = 2 * round_ + rest
+            if 0 < tick - WO_START and rest > 0 and wo_unit - 1 < WO_UNITS:
+                quantise_wo(wo_unit - 1)
+            if 0 <= tick - WO_START and rest < 2 and wo_unit < WO_UNITS:
+                transpose_wo(wo_unit)
+                pair, c = divmod(wo_unit, FEATURE_PASSES)
                 if c == 0 and pair + LOAD_AHEAD < WO_PAIRS:
                     load_wo(pair + LOAD_AHEAD)
 
-            kv, rest = divmod(tick, 2)
-            if rest == 0 and kv + 1 < KV:
+            kv, rest = divmod(tick, PREP_PERIOD)
+            if rest == 1 and kv + 1 < KV:
                 transpose_keys(kv + 1)
                 if kv + 1 + LOAD_AHEAD < KV:
                     load_keys(kv + 1 + LOAD_AHEAD)
-            if rest == 1 and kv < KV:
-                group_values(kv)
-                if kv + LOAD_AHEAD < KV:
-                    load_values(kv + LOAD_AHEAD)
-            if rest == 0 and 0 <= kv - 1 < KV:
+
+            unit, rest = divmod(tick - (TILES - 1) - A_LAG, TILES)
+            if rest == 0 and 0 <= unit < A_UNITS:
+                transpose_a(unit)
+            if rest == 1 and 0 <= unit < A_UNITS:
+                quantise_a(unit)
+
+            unit, rest = divmod(tick - (TILES - 1) - VALUES_LAG, TILES)
+            if rest == 0 and 0 <= unit < A_UNITS:
+                weigh_values(unit)
+
+            panel, half = divmod(tick - PROJECT_START, 2)
+            if 0 <= panel < len(panels):
+                project(*panels[panel], half)
+
+            early = tick - TRANSPOSE_LAG - (HEAD_TILES - 2)
+            if 0 <= early < 2:
+                for n in range(2 * early, 2 * early + 2):
+                    acc = psum_scores.tile([P, PANEL], F32, tag="s")
+                    project_passes(acc, last_row_tile, n, range(FEATURE_PASSES - 2))
+                    last_acc[n] = acc
+            if early == 2:
+                for n in range(PANELS):
+                    project_passes(last_acc[n], last_row_tile, n, range(FEATURE_PASSES - 2, FEATURE_PASSES - 1))
+
+            kv, rest = divmod(tick, PREP_PERIOD)
+            if kv < KV:
+                group_values(kv, rest)
+                if rest == 2:
+                    group_values(kv, 3)
+                    if kv + LOAD_AHEAD < KV:
+                        load_values(kv + LOAD_AHEAD)
+            if rest == 0 and 1 <= kv <= KV:
                 quantise_values(kv - 1)
 
-            if 1 <= tick < Q_UNITS:
-                transpose_queries(tick)
+            if 2 <= tick < 2 * Q_UNITS and tick % 2 == 0:
+                transpose_queries(tick // 2)
 
-        for panel in last_panels:
-            project_passes(last_acc[panel], panel, range(FEATURE_PASSES // 2, FEATURE_PASSES))
-            store_panel(last_acc[panel], panel)
+        for n in range(PANELS):
+            project_passes(last_acc[n], last_row_tile, n, range(FEATURE_PASSES - 1, FEATURE_PASSES))
+            store_panel(last_acc[n], last_row_tile, n)

@@ -33,7 +33,6 @@ KV = BATCH * KV_HEADS
 SLOT_PASSES = SLOTS // K_PASS
 FEATURE_PASSES = FEATURES // K_PASS
 BLOCKS = 2 * PACK
-Q_UNITS = QUERY_TILES * (HEADS // BLOCKS)
 WO_ROWS = 2 * P
 WO_PAIRS = MODEL // WO_ROWS
 WO_UNITS = WO_PAIRS * FEATURE_PASSES
@@ -41,6 +40,7 @@ PANEL = 512
 PANELS = MODEL // PANEL
 
 TILES = K_PASS // HEAD_DIM
+Q_UNITS = QUERY_TILES * FEATURE_PASSES
 A_UNITS = ROW_TILES * FEATURE_PASSES
 HEAD_TILES = A_UNITS * TILES
 LOAD_AHEAD = 2
@@ -54,8 +54,9 @@ VALUES_LAG = QUANTISE_LAG + 1
 A_LAG = VALUES_LAG + 1
 PREP_PERIOD = 3
 WO_START = 5
-PROJECT_START = 42
-LAST_TICK = HEAD_TILES - 1 + A_LAG + 1
+WO_FIRST = 2
+WO_AHEAD = 4
+PROJECT_START = 40
 
 FLOPS = 2 * (2 * BATCH * HEADS * QUERIES * SLOTS * HEAD_DIM) + 2 * BATCH * QUERIES * FEATURES * MODEL
 
@@ -94,8 +95,8 @@ def tile_qwen2dymemdecoderlayer_pa_kernel(tc, q_pos, k_mem, v_mem, Wo, out):
         a_scales = keep.tile([P, ROW_TILES, FEATURE_PASSES * P], U8, align_bytes=64)
 
         q_rows, k_rows, v_rows, v_grouped, wo_rows, wo_grouped = {}, {}, {}, {}, {}, {}
-        score_banks, bank_tops, shifts, e_rows, e_grouped, e_mx = {}, {}, {}, {}, {}, {}
-        row_sums, totals, inverses, a_rows, a_grouped = {}, {}, {}, {}, {}
+        score_banks, bank_tops, shifts, e_rows, e_banks, e_grouped, e_mx = {}, {}, {}, {}, {}, {}, {}
+        row_sums, totals, inverses, o_banks, a_rows, a_banks, a_grouped = {}, {}, {}, {}, {}, {}, {}
         panel_acc, last_acc = {}, {}
 
         def quantise(codes, scales, grouped):
@@ -111,7 +112,7 @@ def tile_qwen2dymemdecoderlayer_pa_kernel(tc, q_pos, k_mem, v_mem, Wo, out):
                 nc.tensor.transpose(out=bank[:, x, :], in_=words[:, x * P : (x + 1) * P], identity=ident_f32[:])
 
         def group_words(copy, bank, grouped):
-            flat = grouped[:].rearrange("p c r t -> p (c r t)")
+            flat = grouped.rearrange("p c r t -> p (c r t)")
             copy(
                 out=flat.bitcast(F32).rearrange("p (c r u) -> p c r u", r=P, u=2),
                 in_=bank[:].rearrange("p (c u) r -> p c r u", u=2),
@@ -119,21 +120,21 @@ def tile_qwen2dymemdecoderlayer_pa_kernel(tc, q_pos, k_mem, v_mem, Wo, out):
             return flat
 
         def load_queries(q_unit):
-            half, query_tile = divmod(q_unit, QUERY_TILES)
-            rows = loads.tile([P, BLOCKS * HEAD_DIM], BF16, tag="q_rows", bufs=Q_UNITS)
+            c, query_tile = divmod(q_unit, QUERY_TILES)
+            rows = loads.tile([P, TILES * HEAD_DIM], BF16, tag="q_rows")
             nc.sync.dma_start(
                 out=rows[:],
-                in_=q_pos[query_tile * P : (query_tile + 1) * P, half * BLOCKS : (half + 1) * BLOCKS, :].rearrange(
+                in_=q_pos[query_tile * P : (query_tile + 1) * P, c * TILES : (c + 1) * TILES, :].rearrange(
                     "q h d -> q (h d)"
                 ),
             )
             q_rows[q_unit] = rows
 
         def transpose_queries(q_unit):
-            half, query_tile = divmod(q_unit, QUERY_TILES)
-            bank = psum_misc.tile([P, BLOCKS, P], BF16, tag="misc")
+            c, query_tile = divmod(q_unit, QUERY_TILES)
+            bank = psum_misc.tile([P, TILES, P], BF16, tag="misc")
             transpose_blocks(bank, q_rows[q_unit])
-            nc.vector.tensor_copy(out=q_t[:, query_tile, half * BLOCKS : (half + 1) * BLOCKS, :], in_=bank[:])
+            nc.vector.tensor_copy(out=q_t[:, query_tile, c * TILES : (c + 1) * TILES, :], in_=bank[:])
 
         def load_keys(kv):
             b, g = divmod(kv, KV_HEADS)
@@ -155,10 +156,10 @@ def tile_qwen2dymemdecoderlayer_pa_kernel(tc, q_pos, k_mem, v_mem, Wo, out):
                 )
             v_rows[kv] = rows
 
-        def transpose_keys(kv):
-            bank = psum_misc.tile([P, BLOCKS, P], BF16, tag="misc")
-            transpose_blocks(bank, k_rows[kv])
-            nc.vector.tensor_copy(out=k_t[:, kv, :], in_=bank[:].rearrange("p x m -> p (x m)"))
+        def transpose_keys(kv, copy, first=0, last=SLOTS):
+            bank = psum_misc.tile([P, (last - first) // P, P], BF16, tag="misc")
+            transpose_blocks(bank, k_rows[kv][:, first:last])
+            copy(out=k_t[:, kv, first:last], in_=bank[:].rearrange("p x m -> p (x m)"))
 
         def group_values(kv, piece):
             if piece == 0:
@@ -178,22 +179,24 @@ def tile_qwen2dymemdecoderlayer_pa_kernel(tc, q_pos, k_mem, v_mem, Wo, out):
         def quantise_values(kv):
             quantise(v_codes[:, kv, :], v_scales[:, kv, :], v_grouped[kv][:].rearrange("p c d t -> p (c d t)"))
 
-        def load_wo(pair):
-            rows = loads.tile([P, 2, FEATURES], BF16, tag="wo_rows")
+        def load_wo(wo_unit):
+            pair, c = divmod(wo_unit, FEATURE_PASSES)
+            rows = loads.tile([P, 2, K_PASS], BF16, tag="wo_rows", bufs=WO_AHEAD + 2)
             nc.sync.dma_start(
-                out=rows[:], in_=Wo[pair * WO_ROWS : (pair + 1) * WO_ROWS, :].rearrange("(y p) a -> p y a", p=P)
+                out=rows[:],
+                in_=Wo[pair * WO_ROWS : (pair + 1) * WO_ROWS, c * K_PASS : (c + 1) * K_PASS].rearrange(
+                    "(y p) a -> p y a", p=P
+                ),
             )
-            wo_rows[pair] = rows
+            wo_rows[wo_unit] = rows
 
         def transpose_wo(wo_unit):
-            pair, c = divmod(wo_unit, FEATURE_PASSES)
             bank = psum_misc.tile([P, 2, WO_ROWS], F32, tag="misc")
             for u in range(2):
-                first = (2 * c + u) * P
                 for y in range(2):
                     nc.tensor.transpose(
                         out=bank[:, u, y * P : (y + 1) * P],
-                        in_=wo_rows[pair][:, y, :].bitcast(F32)[:, first : first + P],
+                        in_=wo_rows[wo_unit][:, y, :].bitcast(F32)[:, u * P : (u + 1) * P],
                         identity=ident_f32[:],
                     )
             grouped = work.tile([P, WO_ROWS * PACK], BF16, tag="wo_grouped", align_bytes=64)
@@ -256,38 +259,51 @@ def tile_qwen2dymemdecoderlayer_pa_kernel(tc, q_pos, k_mem, v_mem, Wo, out):
                 )
             e_rows[i] = e
 
-        def transpose_e(i):
-            bank = psum_misc.tile([P, 2 * SLOT_PASSES, P], F32, tag="misc")
-            transpose_words(bank, e_rows[i][:])
-            grouped = work.tile([P, SLOT_PASSES, P, PACK], BF16, tag="e_grouped", align_bytes=64)
-            e_grouped[i] = group_words(nc.scalar.copy, bank, grouped)
+        def transpose_e(i, first=0, last=SLOT_PASSES):
+            bank = psum_misc.tile([P, 2 * (last - first), P], F32, tag="misc")
+            transpose_words(bank, e_rows[i][:, first * K_PASS : last * K_PASS])
+            e_banks[i, first] = bank
 
-        def quantise_e(i):
-            e_codes = codes_pool.tile([P, SLOT_PASSES * P], U32, tag="e_codes", align_bytes=64)
-            e_scales = codes_pool.tile([P, SLOT_PASSES * P], U8, tag="e_scales", align_bytes=64)
-            quantise(e_codes[:], e_scales[:], e_grouped[i])
-            e_mx[i] = (e_codes, e_scales)
+        def group_e(i, copy, first=0, last=SLOT_PASSES):
+            if first == 0:
+                grouped = work.tile([P, SLOT_PASSES, P, PACK], BF16, tag="e_grouped", align_bytes=64)
+                e_grouped[i] = grouped
+            group_words(copy, e_banks[i, first], e_grouped[i][:, first:last, :, :])
 
-        def add_row_sums(unit):
-            total = small.tile([P, TILES], F32, tag="total")
+        def quantise_e(i, first=0, last=SLOT_PASSES):
+            if first == 0:
+                e_codes = codes_pool.tile([P, SLOT_PASSES * P], U32, tag="e_codes", align_bytes=64)
+                e_scales = codes_pool.tile([P, SLOT_PASSES * P], U8, tag="e_scales", align_bytes=64)
+                e_mx[i] = (e_codes, e_scales)
+            e_codes, e_scales = e_mx[i]
+            cols = slice(first * P, last * P)
+            quantise(e_codes[:, cols], e_scales[:, cols], e_grouped[i][:, first:last, :, :].rearrange("p c r t -> p (c r t)"))
+
+        def add_row_sums(unit, first, last):
+            total = small.tile([P, last - first], F32, tag="total")
             sums = row_sums[unit]
-            nc.gpsimd.tensor_tensor(out=total[:], in0=sums[:, :, 0], in1=sums[:, :, 1], op=ALU.add)
-            totals[unit] = total
+            nc.gpsimd.tensor_tensor(
+                out=total[:], in0=sums[:, first:last, 0], in1=sums[:, first:last, 1], op=ALU.add
+            )
+            totals[unit, first] = total
 
-        def invert_row_sums(unit):
-            inverse = small.tile([P, TILES], F32, tag="inverse")
-            nc.vector.reciprocal(out=inverse[:], in_=totals[unit][:])
-            inverses[unit] = inverse
+        def invert_row_sums(unit, first, last):
+            inverse = small.tile([P, last - first], F32, tag="inverse")
+            nc.vector.reciprocal(out=inverse[:], in_=totals[unit, first][:])
+            inverses[unit, first] = inverse
 
-        def weigh_values(unit):
-            o = psum_misc.tile([P, TILES, HEAD_DIM], F32, tag="misc")
-            for i in range(unit * TILES, (unit + 1) * TILES):
-                kv = place(i)[4]
-                e_codes, e_scales = e_mx[i]
+        def weigh_values(unit, first, last):
+            if first == 0:
+                a = work.tile([P, TILES, HEAD_DIM], BF16, tag="a")
+                a_rows[unit] = a
+            o = psum_misc.tile([P, last - first, HEAD_DIM], F32, tag="misc")
+            for x in range(first, last):
+                kv = place(unit * TILES + x)[4]
+                e_codes, e_scales = e_mx[unit * TILES + x]
                 for c in range(SLOT_PASSES):
                     cols = slice(c * P, (c + 1) * P)
                     nc.tensor.matmul_mx(
-                        out=o[:, i % TILES, :],
+                        out=o[:, x - first, :],
                         lhsT=e_codes[:, cols].bitcast(FP8X4),
                         lhsT_scale=e_scales[:, cols],
                         rhs=v_codes[:, kv, cols].bitcast(FP8X4),
@@ -295,20 +311,29 @@ def tile_qwen2dymemdecoderlayer_pa_kernel(tc, q_pos, k_mem, v_mem, Wo, out):
                         start=(c == 0),
                         stop=(c == SLOT_PASSES - 1),
                     )
-            a = work.tile([P, TILES, HEAD_DIM], BF16, tag="a")
+            o_banks[unit, first] = o
+
+        def divide(unit, first, last):
             nc.vector.tensor_tensor(
-                out=a[:],
-                in0=o[:],
-                in1=inverses[unit][:].unsqueeze(2).broadcast_to([P, TILES, HEAD_DIM]),
+                out=a_rows[unit][:, first:last, :],
+                in0=o_banks[unit, first][:],
+                in1=inverses[unit, first][:].unsqueeze(2).broadcast_to([P, last - first, HEAD_DIM]),
                 op=ALU.mult,
             )
-            a_rows[unit] = a
 
-        def transpose_a(unit):
-            bank = psum_misc.tile([P, 2, P], F32, tag="misc")
-            transpose_words(bank, a_rows[unit][:].rearrange("q x d -> q (x d)"))
-            grouped = work.tile([P, 1, P, PACK], BF16, tag="a_grouped", align_bytes=64)
-            a_grouped[unit] = group_words(nc.vector.tensor_copy, bank, grouped)
+        def transpose_a(unit, first, last):
+            if first == 0:
+                bank = psum_misc.tile([P, 2, P], F32, tag="misc")
+                a_banks[unit] = bank
+            words = a_rows[unit][:].rearrange("q x d -> q (x d)").bitcast(F32)
+            for u in range(2):
+                if first < 2 * (u + 1) <= last:
+                    nc.tensor.transpose(
+                        out=a_banks[unit][:, u, :], in_=words[:, u * P : (u + 1) * P], identity=ident_f32[:]
+                    )
+            if last == TILES:
+                grouped = work.tile([P, 1, P, PACK], BF16, tag="a_grouped", align_bytes=64)
+                a_grouped[unit] = group_words(nc.scalar.copy, a_banks[unit], grouped[:])
 
         def quantise_a(unit):
             row_tile, c = a_order[unit]
@@ -337,6 +362,11 @@ def tile_qwen2dymemdecoderlayer_pa_kernel(tc, q_pos, k_mem, v_mem, Wo, out):
                 out=out[b, query_tile * P : (query_tile + 1) * P, n * PANEL : (n + 1) * PANEL], in_=result[:]
             )
 
+        def start_last_panels(n):
+            acc = psum_scores.tile([P, PANEL], F32, tag="s")
+            project_passes(acc, last_row_tile, n, range(FEATURE_PASSES - 2))
+            last_acc[n] = acc
+
         def project(row_tile, n, half):
             if half == 0:
                 acc = psum_misc.tile([P, PANEL], F32, tag="misc")
@@ -348,82 +378,79 @@ def tile_qwen2dymemdecoderlayer_pa_kernel(tc, q_pos, k_mem, v_mem, Wo, out):
 
         load_keys(0)
         load_queries(0)
+        for wo_unit in range(WO_FIRST):
+            load_wo(wo_unit)
         load_keys(1)
         load_values(0)
         load_queries(1)
         load_values(1)
         load_keys(2)
         load_queries(2)
-        load_queries(3)
-        for pair in range(LOAD_AHEAD):
-            load_wo(pair)
-        transpose_keys(0)
+        for wo_unit in range(WO_FIRST, WO_FIRST + WO_AHEAD):
+            load_wo(wo_unit)
+        transpose_keys(0, nc.scalar.copy, 0, K_PASS)
         transpose_queries(0)
+        transpose_keys(0, nc.scalar.copy, K_PASS, SLOTS)
 
         panels = [(row_tile, n) for n in range(PANELS) for row_tile in range(QUERY_TILES)]
         panels += [(row_tile, n) for row_tile in range(QUERY_TILES, ROW_TILES - 1) for n in range(PANELS)]
         last_row_tile = ROW_TILES - 1
-        for tick in range(LAST_TICK + 1):
-            if tick < HEAD_TILES:
-                scores(tick)
-                find_shift(tick)
+        for tick in range(HEAD_TILES):
+            scores(tick)
+            find_shift(tick)
 
-            if 0 <= tick - EXP_LAG < HEAD_TILES:
+            if tick >= EXP_LAG:
                 exponentials(tick - EXP_LAG)
 
-            if 0 <= tick - TRANSPOSE_LAG < HEAD_TILES:
+            if tick >= TRANSPOSE_LAG:
                 transpose_e(tick - TRANSPOSE_LAG)
+                group_e(tick - TRANSPOSE_LAG, nc.scalar.copy)
 
-            if 0 <= tick - QUANTISE_LAG < HEAD_TILES:
+            if tick >= QUANTISE_LAG:
                 quantise_e(tick - QUANTISE_LAG)
 
             unit, rest = divmod(tick - (TILES - 1) - SUM_LAG, TILES)
-            if rest == 0 and 0 <= unit < A_UNITS:
-                add_row_sums(unit)
+            if rest == 0 and 0 <= unit:
+                add_row_sums(unit, 0, TILES)
 
             unit, rest = divmod(tick - (TILES - 1) - INVERT_LAG, TILES)
-            if rest == 0 and 0 <= unit < A_UNITS:
-                invert_row_sums(unit)
+            if rest == 0 and 0 <= unit:
+                invert_row_sums(unit, 0, TILES)
 
+            unit, rest = divmod(tick - (TILES - 1) - A_LAG, TILES)
+            if rest == 0 and 0 <= unit:
+                transpose_a(unit, 0, TILES)
+            if rest == 1 and 0 <= unit:
+                quantise_a(unit)
+
+            if tick == 0:
+                for wo_unit in range(WO_FIRST):
+                    transpose_wo(wo_unit)
+            if 1 <= tick <= WO_FIRST:
+                quantise_wo(tick - 1)
             round_, rest = divmod(tick - WO_START, PREP_PERIOD)
-            wo_unit = 2 * round_ + rest
-            if 0 < tick - WO_START and rest > 0 and wo_unit - 1 < WO_UNITS:
+            wo_unit = WO_FIRST + 2 * round_ + rest
+            if 0 <= tick - WO_START and rest > 0 and wo_unit - 1 < WO_UNITS:
                 quantise_wo(wo_unit - 1)
             if 0 <= tick - WO_START and rest < 2 and wo_unit < WO_UNITS:
                 transpose_wo(wo_unit)
-                pair, c = divmod(wo_unit, FEATURE_PASSES)
-                if c == 0 and pair + LOAD_AHEAD < WO_PAIRS:
-                    load_wo(pair + LOAD_AHEAD)
+                if wo_unit + WO_AHEAD < WO_UNITS:
+                    load_wo(wo_unit + WO_AHEAD)
 
             kv, rest = divmod(tick, PREP_PERIOD)
             if rest == 1 and kv + 1 < KV:
-                transpose_keys(kv + 1)
+                transpose_keys(kv + 1, nc.vector.tensor_copy)
                 if kv + 1 + LOAD_AHEAD < KV:
                     load_keys(kv + 1 + LOAD_AHEAD)
-
-            unit, rest = divmod(tick - (TILES - 1) - A_LAG, TILES)
-            if rest == 0 and 0 <= unit < A_UNITS:
-                transpose_a(unit)
-            if rest == 1 and 0 <= unit < A_UNITS:
-                quantise_a(unit)
-
-            unit, rest = divmod(tick - (TILES - 1) - VALUES_LAG, TILES)
-            if rest == 0 and 0 <= unit < A_UNITS:
-                weigh_values(unit)
 
             panel, half = divmod(tick - PROJECT_START, 2)
             if 0 <= panel < len(panels):
                 project(*panels[panel], half)
 
-            early = tick - TRANSPOSE_LAG - (HEAD_TILES - 2)
-            if 0 <= early < 2:
-                for n in range(2 * early, 2 * early + 2):
-                    acc = psum_scores.tile([P, PANEL], F32, tag="s")
-                    project_passes(acc, last_row_tile, n, range(FEATURE_PASSES - 2))
-                    last_acc[n] = acc
-            if early == 2:
-                for n in range(PANELS):
-                    project_passes(last_acc[n], last_row_tile, n, range(FEATURE_PASSES - 2, FEATURE_PASSES - 1))
+            unit, rest = divmod(tick - (TILES - 1) - VALUES_LAG, TILES)
+            if rest == 0 and 0 <= unit:
+                weigh_values(unit, 0, TILES)
+                divide(unit, 0, TILES)
 
             kv, rest = divmod(tick, PREP_PERIOD)
             if kv < KV:
@@ -435,9 +462,43 @@ def tile_qwen2dymemdecoderlayer_pa_kernel(tc, q_pos, k_mem, v_mem, Wo, out):
             if rest == 0 and 1 <= kv <= KV:
                 quantise_values(kv - 1)
 
-            if 2 <= tick < 2 * Q_UNITS and tick % 2 == 0:
-                transpose_queries(tick // 2)
+            if rest == 0 and tick // PREP_PERIOD + 1 < Q_UNITS:
+                q_unit = tick // PREP_PERIOD + 1
+                transpose_queries(q_unit)
+                if q_unit + LOAD_AHEAD < Q_UNITS:
+                    load_queries(q_unit + LOAD_AHEAD)
 
+        unit, x, i = A_UNITS - 1, TILES - 1, HEAD_TILES - 1
+        quantise_e(i - 2)
+        exponentials(i)
+        transpose_e(i - 1)
+        group_e(i - 1, nc.vector.tensor_copy)
+        transpose_a(unit - 1, 0, TILES)
+        start_last_panels(0)
+        start_last_panels(1)
+        transpose_e(i, 0, 1)
+        group_e(i, nc.vector.tensor_copy, 0, 1)
+        quantise_e(i - 1)
+        transpose_e(i, 1, 2)
+        group_e(i, nc.scalar.copy, 1, 2)
+        quantise_a(unit - 1)
+        add_row_sums(unit, 0, x)
+        invert_row_sums(unit, 0, x)
+        quantise_e(i, 0, 1)
+        weigh_values(unit, 0, x)
+        start_last_panels(2)
+        add_row_sums(unit, x, TILES)
+        quantise_e(i, 1, 2)
+        divide(unit, 0, x)
+        invert_row_sums(unit, x, TILES)
+        weigh_values(unit, x, TILES)
+        start_last_panels(3)
+        transpose_a(unit, 0, x)
+        divide(unit, x, TILES)
+        transpose_a(unit, x, TILES)
+        for n in range(PANELS):
+            project_passes(last_acc[n], last_row_tile, n, range(FEATURE_PASSES - 2, FEATURE_PASSES - 1))
+        quantise_a(unit)
         for n in range(PANELS):
             project_passes(last_acc[n], last_row_tile, n, range(FEATURE_PASSES - 1, FEATURE_PASSES))
             store_panel(last_acc[n], last_row_tile, n)

@@ -43,7 +43,7 @@ TILES = K_PASS // HEAD_DIM
 Q_UNITS = QUERY_TILES * FEATURE_PASSES
 A_UNITS = ROW_TILES * FEATURE_PASSES
 HEAD_TILES = A_UNITS * TILES
-LOAD_AHEAD = 2
+LOAD_AHEAD = 4
 
 EXP_LAG = 1
 TRANSPOSE_LAG = 2
@@ -55,7 +55,6 @@ A_LAG = VALUES_LAG + 1
 PREP_PERIOD = 3
 WO_START = 5
 WO_FIRST = 2
-WO_AHEAD = 4
 PROJECT_START = 40
 
 FLOPS = 2 * (2 * BATCH * HEADS * QUERIES * SLOTS * HEAD_DIM) + 2 * BATCH * QUERIES * FEATURES * MODEL
@@ -119,6 +118,13 @@ def tile_qwen2dymemdecoderlayer_pa_kernel(tc, q_pos, k_mem, v_mem, Wo, out):
             )
             return flat
 
+        def warm_up():
+            zeros = keep.tile([P, PANEL], BF16)
+            nc.vector.memset(zeros[:], 0.0)
+            bank = psum_misc.tile([P, PANEL], F32, tag="misc")
+            for turn in range(6):
+                nc.tensor.matmul(out=bank[:], lhsT=zeros[:, :P], rhs=zeros[:], start=True, stop=True)
+
         def load_queries(q_unit):
             c, query_tile = divmod(q_unit, QUERY_TILES)
             rows = loads.tile([P, TILES * HEAD_DIM], BF16, tag="q_rows")
@@ -181,7 +187,7 @@ def tile_qwen2dymemdecoderlayer_pa_kernel(tc, q_pos, k_mem, v_mem, Wo, out):
 
         def load_wo(wo_unit):
             pair, c = divmod(wo_unit, FEATURE_PASSES)
-            rows = loads.tile([P, 2, K_PASS], BF16, tag="wo_rows", bufs=WO_AHEAD + 2)
+            rows = loads.tile([P, 2, K_PASS], BF16, tag="wo_rows", bufs=LOAD_AHEAD + 2)
             nc.sync.dma_start(
                 out=rows[:],
                 in_=Wo[pair * WO_ROWS : (pair + 1) * WO_ROWS, c * K_PASS : (c + 1) * K_PASS].rearrange(
@@ -333,7 +339,7 @@ def tile_qwen2dymemdecoderlayer_pa_kernel(tc, q_pos, k_mem, v_mem, Wo, out):
                     )
             if last == TILES:
                 grouped = work.tile([P, 1, P, PACK], BF16, tag="a_grouped", align_bytes=64)
-                a_grouped[unit] = group_words(nc.scalar.copy, a_banks[unit], grouped[:])
+                a_grouped[unit] = group_words(nc.vector.tensor_copy, a_banks[unit], grouped[:])
 
         def quantise_a(unit):
             row_tile, c = a_order[unit]
@@ -353,10 +359,9 @@ def tile_qwen2dymemdecoderlayer_pa_kernel(tc, q_pos, k_mem, v_mem, Wo, out):
                     stop=(c == FEATURE_PASSES - 1),
                 )
 
-        def store_panel(acc, row_tile, n):
+        def store_panel(acc, row_tile, n, copy):
             b, query_tile = divmod(row_tile, QUERY_TILES)
             result = work.tile([P, PANEL], F32, tag="result", bufs=PANELS)
-            copy = nc.scalar.copy if n % 4 == 3 else nc.vector.tensor_copy
             copy(out=result[:], in_=acc[:])
             nc.sync.dma_start(
                 out=out[b, query_tile * P : (query_tile + 1) * P, n * PANEL : (n + 1) * PANEL], in_=result[:]
@@ -367,27 +372,25 @@ def tile_qwen2dymemdecoderlayer_pa_kernel(tc, q_pos, k_mem, v_mem, Wo, out):
             project_passes(acc, last_row_tile, n, range(FEATURE_PASSES - 2))
             last_acc[n] = acc
 
-        def project(row_tile, n, half):
+        def project(row_tile, n, half, copy):
             if half == 0:
                 acc = psum_misc.tile([P, PANEL], F32, tag="misc")
                 panel_acc[row_tile, n] = acc
             acc = panel_acc[row_tile, n]
             project_passes(acc, row_tile, n, range(half * FEATURE_PASSES // 2, (half + 1) * FEATURE_PASSES // 2))
             if half == 1:
-                store_panel(acc, row_tile, n)
+                store_panel(acc, row_tile, n, copy)
 
         load_keys(0)
         load_queries(0)
         for wo_unit in range(WO_FIRST):
             load_wo(wo_unit)
-        load_keys(1)
-        load_values(0)
-        load_queries(1)
-        load_values(1)
-        load_keys(2)
-        load_queries(2)
-        for wo_unit in range(WO_FIRST, WO_FIRST + WO_AHEAD):
-            load_wo(wo_unit)
+        for n in range(1, LOAD_AHEAD + 1):
+            load_keys(n)
+            load_values(n - 1)
+            load_queries(n)
+            load_wo(WO_FIRST + n - 1)
+        warm_up()
         transpose_keys(0, nc.scalar.copy, 0, K_PASS)
         transpose_queries(0)
         transpose_keys(0, nc.scalar.copy, K_PASS, SLOTS)
@@ -423,6 +426,13 @@ def tile_qwen2dymemdecoderlayer_pa_kernel(tc, q_pos, k_mem, v_mem, Wo, out):
             if rest == 1 and 0 <= unit:
                 quantise_a(unit)
 
+            kv, rest = divmod(tick, PREP_PERIOD)
+            kv += 1
+            if (rest == 1 or tick == 0) and tick != 1 and kv < KV:
+                transpose_keys(kv, nc.vector.tensor_copy)
+                if kv + LOAD_AHEAD < KV:
+                    load_keys(kv + LOAD_AHEAD)
+
             if tick == 0:
                 for wo_unit in range(WO_FIRST):
                     transpose_wo(wo_unit)
@@ -430,22 +440,16 @@ def tile_qwen2dymemdecoderlayer_pa_kernel(tc, q_pos, k_mem, v_mem, Wo, out):
                 quantise_wo(tick - 1)
             round_, rest = divmod(tick - WO_START, PREP_PERIOD)
             wo_unit = WO_FIRST + 2 * round_ + rest
-            if 0 <= tick - WO_START and rest > 0 and wo_unit - 1 < WO_UNITS:
+            if rest < 2 and WO_FIRST < wo_unit <= WO_UNITS:
                 quantise_wo(wo_unit - 1)
-            if 0 <= tick - WO_START and rest < 2 and wo_unit < WO_UNITS:
+            if rest < 2 and WO_FIRST <= wo_unit < WO_UNITS:
                 transpose_wo(wo_unit)
-                if wo_unit + WO_AHEAD < WO_UNITS:
-                    load_wo(wo_unit + WO_AHEAD)
-
-            kv, rest = divmod(tick, PREP_PERIOD)
-            if rest == 1 and kv + 1 < KV:
-                transpose_keys(kv + 1, nc.vector.tensor_copy)
-                if kv + 1 + LOAD_AHEAD < KV:
-                    load_keys(kv + 1 + LOAD_AHEAD)
+                if wo_unit + LOAD_AHEAD < WO_UNITS:
+                    load_wo(wo_unit + LOAD_AHEAD)
 
             panel, half = divmod(tick - PROJECT_START, 2)
             if 0 <= panel < len(panels):
-                project(*panels[panel], half)
+                project(*panels[panel], half, nc.vector.tensor_copy if panel % 2 == 0 else nc.scalar.copy)
 
             unit, rest = divmod(tick - (TILES - 1) - VALUES_LAG, TILES)
             if rest == 0 and 0 <= unit:
@@ -462,8 +466,9 @@ def tile_qwen2dymemdecoderlayer_pa_kernel(tc, q_pos, k_mem, v_mem, Wo, out):
             if rest == 0 and 1 <= kv <= KV:
                 quantise_values(kv - 1)
 
-            if rest == 0 and tick // PREP_PERIOD + 1 < Q_UNITS:
-                q_unit = tick // PREP_PERIOD + 1
+            q_unit, rest = divmod(tick, PREP_PERIOD)
+            q_unit += 1
+            if rest == 2 and q_unit < Q_UNITS:
                 transpose_queries(q_unit)
                 if q_unit + LOAD_AHEAD < Q_UNITS:
                     load_queries(q_unit + LOAD_AHEAD)
@@ -473,8 +478,8 @@ def tile_qwen2dymemdecoderlayer_pa_kernel(tc, q_pos, k_mem, v_mem, Wo, out):
         exponentials(i)
         transpose_e(i - 1)
         group_e(i - 1, nc.vector.tensor_copy)
-        transpose_a(unit - 1, 0, TILES)
         start_last_panels(0)
+        transpose_a(unit - 1, 0, TILES)
         start_last_panels(1)
         transpose_e(i, 0, 1)
         group_e(i, nc.vector.tensor_copy, 0, 1)
@@ -501,4 +506,4 @@ def tile_qwen2dymemdecoderlayer_pa_kernel(tc, q_pos, k_mem, v_mem, Wo, out):
         quantise_a(unit)
         for n in range(PANELS):
             project_passes(last_acc[n], last_row_tile, n, range(FEATURE_PASSES - 1, FEATURE_PASSES))
-            store_panel(last_acc[n], last_row_tile, n)
+            store_panel(last_acc[n], last_row_tile, n, nc.vector.tensor_copy if n % 2 == 0 else nc.scalar.copy)

@@ -44,6 +44,7 @@ Q_UNITS = QUERY_TILES * FEATURE_PASSES
 A_UNITS = ROW_TILES * FEATURE_PASSES
 HEAD_TILES = A_UNITS * TILES
 LOAD_AHEAD = 4
+PAIRS_AHEAD = 2
 
 EXP_LAG = 1
 TRANSPOSE_LAG = 2
@@ -53,6 +54,7 @@ INVERT_LAG = SUM_LAG + 1
 VALUES_LAG = QUANTISE_LAG + 1
 A_LAG = VALUES_LAG + 1
 PREP_PERIOD = 3
+VALUES_START = 2
 WO_START = 5
 WO_FIRST = 2
 PROJECT_START = 40
@@ -142,52 +144,55 @@ def tile_qwen2dymemdecoderlayer_pa_kernel(tc, q_pos, k_mem, v_mem, Wo, out):
             transpose_blocks(bank, q_rows[q_unit])
             nc.vector.tensor_copy(out=q_t[:, query_tile, c * TILES : (c + 1) * TILES, :], in_=bank[:])
 
-        def load_keys(kv):
-            b, g = divmod(kv, KV_HEADS)
-            rows = loads.tile([P, BLOCKS * HEAD_DIM], BF16, tag="k_rows")
+        def load_slots(source, tag, pair):
+            b, first = divmod(GROUP * pair, KV_HEADS)
+            rows = loads.tile([P, SLOT_PASSES, PACK, GROUP, HEAD_DIM], BF16, tag=tag, bufs=PAIRS_AHEAD + 1)
             for c in range(SLOT_PASSES):
                 nc.sync.dma_start(
-                    out=rows[:, c * K_PASS : (c + 1) * K_PASS].rearrange("p (t d) -> p t d", t=PACK),
-                    in_=k_mem[b, c * K_PASS : (c + 1) * K_PASS, g, :].rearrange("(p t) d -> p t d", t=PACK),
+                    out=rows[:, c, :, :, :].rearrange("p t g d -> p t (g d)"),
+                    in_=source[b, c * K_PASS : (c + 1) * K_PASS, first : first + GROUP, :].rearrange(
+                        "(p t) g d -> p t (g d)", t=PACK
+                    ),
                 )
-            k_rows[kv] = rows
+            return rows
 
-        def load_values(kv):
-            b, g = divmod(kv, KV_HEADS)
-            rows = loads.tile([P, SLOT_PASSES, PACK, HEAD_DIM], BF16, tag="v_rows")
-            for c in range(SLOT_PASSES):
-                nc.sync.dma_start(
-                    out=rows[:, c, :, :],
-                    in_=v_mem[b, c * K_PASS : (c + 1) * K_PASS, g, :].rearrange("(p t) d -> p t d", t=PACK),
+        def load_keys(pair):
+            rows = load_slots(k_mem, "k_rows", pair)
+            for j in range(GROUP):
+                k_rows[GROUP * pair + j] = rows[:, :, :, j, :]
+
+        def load_values(pair):
+            rows = load_slots(v_mem, "v_rows", pair)
+            for j in range(GROUP):
+                v_rows[GROUP * pair + j] = rows[:, :, :, j, :]
+
+        def transpose_keys(kv, copy, first=0, last=SLOT_PASSES):
+            bank = psum_misc.tile([P, (last - first) * PACK, P], BF16, tag="misc")
+            for x in range((last - first) * PACK):
+                nc.tensor.transpose(
+                    out=bank[:, x, :], in_=k_rows[kv][:, first + x // PACK, x % PACK, :], identity=ident_bf16[:]
                 )
-            v_rows[kv] = rows
+            copy(out=k_t[:, kv, first * K_PASS : last * K_PASS], in_=bank[:].rearrange("p x m -> p (x m)"))
 
-        def transpose_keys(kv, copy, first=0, last=SLOTS):
-            bank = psum_misc.tile([P, (last - first) // P, P], BF16, tag="misc")
-            transpose_blocks(bank, k_rows[kv][:, first:last])
-            copy(out=k_t[:, kv, first:last], in_=bank[:].rearrange("p x m -> p (x m)"))
-
-        def group_values(kv, piece):
-            if piece == 0:
-                grouped = work.tile([P, SLOT_PASSES, HEAD_DIM, PACK], BF16, tag="v_grouped", align_bytes=64)
-                v_grouped[kv] = grouped
-            c, half = divmod(piece, 2)
-            d = slice(half * (HEAD_DIM // 2), (half + 1) * (HEAD_DIM // 2))
+        def group_values(kv, c):
+            grouped = work.tile([P, HEAD_DIM, PACK], BF16, tag=("v_first", "v_second")[c], bufs=1, align_bytes=64)
             nc.gpsimd.tensor_scalar(
-                out=v_grouped[kv][:, c, d, :],
-                in0=v_rows[kv][:, c, :, d].rearrange("p t d -> p d t"),
+                out=grouped[:],
+                in0=v_rows[kv][:, c, :, :].rearrange("p t d -> p d t"),
                 scalar1=1.0,
                 scalar2=0.0,
                 op0=ALU.mult,
                 op1=ALU.add,
             )
+            v_grouped[kv, c] = grouped
 
-        def quantise_values(kv):
-            quantise(v_codes[:, kv, :], v_scales[:, kv, :], v_grouped[kv][:].rearrange("p c d t -> p (c d t)"))
+        def quantise_values(kv, c):
+            cols = slice(c * HEAD_DIM, (c + 1) * HEAD_DIM)
+            quantise(v_codes[:, kv, cols], v_scales[:, kv, cols], v_grouped[kv, c][:].rearrange("p d t -> p (d t)"))
 
         def load_wo(wo_unit):
             pair, c = divmod(wo_unit, FEATURE_PASSES)
-            rows = loads.tile([P, 2, K_PASS], BF16, tag="wo_rows", bufs=LOAD_AHEAD + 2)
+            rows = loads.tile([P, 2, K_PASS], BF16, tag="wo_rows", bufs=LOAD_AHEAD + WO_FIRST)
             nc.sync.dma_start(
                 out=rows[:],
                 in_=Wo[pair * WO_ROWS : (pair + 1) * WO_ROWS, c * K_PASS : (c + 1) * K_PASS].rearrange(
@@ -381,26 +386,41 @@ def tile_qwen2dymemdecoderlayer_pa_kernel(tc, q_pos, k_mem, v_mem, Wo, out):
             if half == 1:
                 store_panel(acc, row_tile, n, copy)
 
-        load_keys(0)
         load_queries(0)
+        load_keys(0)
         for wo_unit in range(WO_FIRST):
             load_wo(wo_unit)
+        load_values(0)
         for n in range(1, LOAD_AHEAD + 1):
-            load_keys(n)
-            load_values(n - 1)
             load_queries(n)
             load_wo(WO_FIRST + n - 1)
+            if n <= PAIRS_AHEAD:
+                load_keys(n)
+                load_values(n)
         warm_up()
-        transpose_keys(0, nc.scalar.copy, 0, K_PASS)
+        transpose_keys(0, nc.scalar.copy, 0, 1)
         transpose_queries(0)
-        transpose_keys(0, nc.scalar.copy, K_PASS, SLOTS)
+        transpose_keys(0, nc.scalar.copy, 1, 2)
+        transpose_wo(0)
 
         panels = [(row_tile, n) for n in range(PANELS) for row_tile in range(QUERY_TILES)]
         panels += [(row_tile, n) for row_tile in range(QUERY_TILES, ROW_TILES - 1) for n in range(PANELS)]
         last_row_tile = ROW_TILES - 1
         for tick in range(HEAD_TILES):
+            kv, c = divmod(tick - VALUES_START, PREP_PERIOD)
+            if c < SLOT_PASSES and 0 <= kv < KV:
+                quantise_values(kv, c)
+                if kv + 1 < KV:
+                    group_values(kv + 1, c)
+                pair = (kv + 1) // GROUP + PAIRS_AHEAD + 1
+                if c == SLOT_PASSES - 1 and (kv + 1) % GROUP == GROUP - 1 and pair < KV // GROUP:
+                    load_values(pair)
+
             scores(tick)
             find_shift(tick)
+
+            if tick < SLOT_PASSES:
+                group_values(0, tick)
 
             if tick >= EXP_LAG:
                 exponentials(tick - EXP_LAG)
@@ -423,29 +443,24 @@ def tile_qwen2dymemdecoderlayer_pa_kernel(tc, q_pos, k_mem, v_mem, Wo, out):
             unit, rest = divmod(tick - (TILES - 1) - A_LAG, TILES)
             if rest == 0 and 0 <= unit:
                 transpose_a(unit, 0, TILES)
-            if rest == 1 and 0 <= unit:
-                quantise_a(unit)
+
+            if tick == 0:
+                for wo_unit in range(1, WO_FIRST):
+                    transpose_wo(wo_unit)
+            round_, rest = divmod(tick - WO_START, PREP_PERIOD)
+            wo_unit = WO_FIRST + 2 * round_ + rest
+            if rest < 2 and WO_FIRST <= wo_unit < WO_UNITS:
+                transpose_wo(wo_unit)
+                if wo_unit + LOAD_AHEAD < WO_UNITS:
+                    load_wo(wo_unit + LOAD_AHEAD)
 
             kv, rest = divmod(tick, PREP_PERIOD)
             kv += 1
             if (rest == 1 or tick == 0) and tick != 1 and kv < KV:
                 transpose_keys(kv, nc.vector.tensor_copy)
-                if kv + LOAD_AHEAD < KV:
-                    load_keys(kv + LOAD_AHEAD)
-
-            if tick == 0:
-                for wo_unit in range(WO_FIRST):
-                    transpose_wo(wo_unit)
-            if 1 <= tick <= WO_FIRST:
-                quantise_wo(tick - 1)
-            round_, rest = divmod(tick - WO_START, PREP_PERIOD)
-            wo_unit = WO_FIRST + 2 * round_ + rest
-            if rest < 2 and WO_FIRST < wo_unit <= WO_UNITS:
-                quantise_wo(wo_unit - 1)
-            if rest < 2 and WO_FIRST <= wo_unit < WO_UNITS:
-                transpose_wo(wo_unit)
-                if wo_unit + LOAD_AHEAD < WO_UNITS:
-                    load_wo(wo_unit + LOAD_AHEAD)
+                pair = kv // GROUP + PAIRS_AHEAD + 1
+                if kv % GROUP == GROUP - 1 and pair < KV // GROUP:
+                    load_keys(pair)
 
             panel, half = divmod(tick - PROJECT_START, 2)
             if 0 <= panel < len(panels):
@@ -456,22 +471,23 @@ def tile_qwen2dymemdecoderlayer_pa_kernel(tc, q_pos, k_mem, v_mem, Wo, out):
                 weigh_values(unit, 0, TILES)
                 divide(unit, 0, TILES)
 
-            kv, rest = divmod(tick, PREP_PERIOD)
-            if kv < KV:
-                group_values(kv, rest)
-                if rest == 2:
-                    group_values(kv, 3)
-                    if kv + LOAD_AHEAD < KV:
-                        load_values(kv + LOAD_AHEAD)
-            if rest == 0 and 1 <= kv <= KV:
-                quantise_values(kv - 1)
-
             q_unit, rest = divmod(tick, PREP_PERIOD)
             q_unit += 1
             if rest == 2 and q_unit < Q_UNITS:
                 transpose_queries(q_unit)
                 if q_unit + LOAD_AHEAD < Q_UNITS:
                     load_queries(q_unit + LOAD_AHEAD)
+
+            unit, rest = divmod(tick - (TILES - 1) - A_LAG, TILES)
+            if rest == 1 and 0 <= unit:
+                quantise_a(unit)
+
+            if 1 <= tick <= WO_FIRST:
+                quantise_wo(tick - 1)
+            round_, rest = divmod(tick - WO_START, PREP_PERIOD)
+            wo_unit = WO_FIRST + 2 * round_ + rest
+            if rest < 2 and WO_FIRST < wo_unit <= WO_UNITS:
+                quantise_wo(wo_unit - 1)
 
         unit, x, i = A_UNITS - 1, TILES - 1, HEAD_TILES - 1
         quantise_e(i - 2)

@@ -344,7 +344,7 @@ def tile_qwen2dymemdecoderlayer_pa_kernel(tc, q_pos, k_mem, v_mem, Wo, out):
                     )
             if last == TILES:
                 grouped = work.tile([P, 1, P, PACK], BF16, tag="a_grouped", align_bytes=64)
-                a_grouped[unit] = group_words(nc.vector.tensor_copy, a_banks[unit], grouped[:])
+                a_grouped[unit] = group_words(nc.scalar.copy, a_banks[unit], grouped[:])
 
         def quantise_a(unit):
             row_tile, c = a_order[unit]

@@ -52,7 +52,8 @@ QUANTISE_LAG = 3
 SUM_LAG = EXP_LAG + 1
 INVERT_LAG = SUM_LAG + 1
 VALUES_LAG = QUANTISE_LAG + 1
-A_LAG = VALUES_LAG + 1
+DIVIDE_LAG = VALUES_LAG + 1
+A_LAG = DIVIDE_LAG + 1
 PREP_PERIOD = 3
 VALUES_START = 2
 WO_START = 5
@@ -419,6 +420,10 @@ def tile_qwen2dymemdecoderlayer_pa_kernel(tc, q_pos, k_mem, v_mem, Wo, out):
             scores(tick)
             find_shift(tick)
 
+            unit, rest = divmod(tick - (TILES - 1) - DIVIDE_LAG, TILES)
+            if rest == 0 and 0 <= unit:
+                divide(unit, 0, TILES)
+
             if tick < SLOT_PASSES:
                 group_values(0, tick)
 
@@ -469,7 +474,6 @@ def tile_qwen2dymemdecoderlayer_pa_kernel(tc, q_pos, k_mem, v_mem, Wo, out):
             unit, rest = divmod(tick - (TILES - 1) - VALUES_LAG, TILES)
             if rest == 0 and 0 <= unit:
                 weigh_values(unit, 0, TILES)
-                divide(unit, 0, TILES)
 
             q_unit, rest = divmod(tick, PREP_PERIOD)
             q_unit += 1
@@ -490,6 +494,7 @@ def tile_qwen2dymemdecoderlayer_pa_kernel(tc, q_pos, k_mem, v_mem, Wo, out):
                 quantise_wo(wo_unit - 1)
 
         unit, x, i = A_UNITS - 1, TILES - 1, HEAD_TILES - 1
+        divide(unit - 1, 0, TILES)
         quantise_e(i - 2)
         exponentials(i)
         transpose_e(i - 1)

@@ -235,6 +235,14 @@ def tile_qwen2dymemdecoderlayer_pa_kernel(tc, q_pos, k_mem, v_mem, Wo, out):
             tops = small.tile([P, SLOT_PASSES], F32, tag="tops")
             for c in range(SLOT_PASSES):
                 s = psum_scores.tile([P, K_PASS], F32, tag="s")
+                if c == 0:
+                    nc.tensor.matmul(
+                        out=s[:, :128],
+                        lhsT=q_t[:, row_tile % QUERY_TILES, head, :],
+                        rhs=k_t[:, kv, :128],
+                        start=True,
+                        stop=True,
+                    )
                 nc.tensor.matmul(
                     out=s[:],
                     lhsT=q_t[:, row_tile % QUERY_TILES, head, :],
@@ -502,22 +510,22 @@ def tile_qwen2dymemdecoderlayer_pa_kernel(tc, q_pos, k_mem, v_mem, Wo, out):
         start_last_panels(0)
         transpose_a(unit - 1, 0, TILES)
         start_last_panels(1)
+        quantise_e(i - 1)
         transpose_e(i, 0, 1)
         group_e(i, nc.vector.tensor_copy, 0, 1)
-        quantise_e(i - 1)
         transpose_e(i, 1, 2)
         group_e(i, nc.scalar.copy, 1, 2)
-        quantise_a(unit - 1)
         add_row_sums(unit, 0, x)
-        invert_row_sums(unit, 0, x)
         quantise_e(i, 0, 1)
         weigh_values(unit, 0, x)
         start_last_panels(2)
         add_row_sums(unit, x, TILES)
         quantise_e(i, 1, 2)
+        weigh_values(unit, x, TILES)
+        invert_row_sums(unit, 0, x)
+        quantise_a(unit - 1)
         divide(unit, 0, x)
         invert_row_sums(unit, x, TILES)
-        weigh_values(unit, x, TILES)
         start_last_panels(3)
         transpose_a(unit, 0, x)
         divide(unit, x, TILES)

from contextlib import ExitStack

import concourse.masks as masks
import concourse.mybir as mybir

BF16 = mybir.dt.bfloat16
F32 = mybir.dt.float32
U32 = mybir.dt.uint32
U8 = mybir.dt.uint8
FP8X4 = mybir.dt.float8_e4m3fn_x4
EXP = mybir.ActivationFunctionType.Exp
ALU = mybir.AluOpType
ALONG_ROW = mybir.AxisListType.X

P = 128
PACK = 4
K_PASS = P * PACK

BATCH = 2
QUERIES = 256
SLOTS = 1024
HEADS = 16
KV_HEADS = 8
GROUP = HEADS // KV_HEADS
HEAD_DIM = 128
FEATURES = HEADS * HEAD_DIM
MODEL = 2048
SCORE_FACTOR = 0.5

QUERY_TILES = QUERIES // P
ROW_TILES = BATCH * QUERY_TILES
KV = BATCH * KV_HEADS
SLOT_PASSES = SLOTS // K_PASS
FEATURE_PASSES = FEATURES // K_PASS
BLOCKS = 2 * PACK
WO_ROWS = 2 * P
WO_PAIRS = MODEL // WO_ROWS
WO_UNITS = WO_PAIRS * FEATURE_PASSES
PANEL = 512
PANELS = MODEL // PANEL

TILES = K_PASS // HEAD_DIM
Q_UNITS = QUERY_TILES * FEATURE_PASSES
A_UNITS = ROW_TILES * FEATURE_PASSES
HEAD_TILES = A_UNITS * TILES
LOAD_AHEAD = 4
PAIRS_AHEAD = 2

EXP_LAG = 1
TRANSPOSE_LAG = 2
QUANTISE_LAG = 3
SUM_LAG = EXP_LAG + 1
INVERT_LAG = SUM_LAG + 1
VALUES_LAG = QUANTISE_LAG + 1
DIVIDE_LAG = VALUES_LAG + 1
A_LAG = DIVIDE_LAG + 1
PREP_PERIOD = 3
VALUES_START = 2
WO_START = 5
WO_FIRST = 2
PROJECT_START = 40

FLOPS = 2 * (2 * BATCH * HEADS * QUERIES * SLOTS * HEAD_DIM) + 2 * BATCH * QUERIES * FEATURES * MODEL


def a_unit_order():
    first = [(query_tile, c) for c in range(FEATURE_PASSES) for query_tile in range(QUERY_TILES)]
    second = [(QUERY_TILES + query_tile, c) for query_tile in range(QUERY_TILES) for c in range(FEATURE_PASSES)]
    return first + second


def tile_qwen2dymemdecoderlayer_pa_kernel(tc, q_pos, k_mem, v_mem, Wo, out):
    nc = tc.nc
    a_order = a_unit_order()
    with ExitStack() as ctx:
        keep = ctx.enter_context(tc.tile_pool(name="keep", bufs=1))
        loads = ctx.enter_context(tc.tile_pool(name="loads", bufs=LOAD_AHEAD + 1))
        work = ctx.enter_context(tc.tile_pool(name="work", bufs=3))
        codes_pool = ctx.enter_context(tc.tile_pool(name="codes", bufs=TILES + VALUES_LAG))
        small = ctx.enter_context(tc.tile_pool(name="small", bufs=4))
        psum_scores = ctx.enter_context(tc.psum_pool(name="psum_scores", bufs=2 * SLOT_PASSES))
        psum_misc = ctx.enter_context(tc.psum_pool(name="psum_misc", bufs=4))
        ctx.enter_context(tc.manual_schedule())

        ident_bf16 = keep.tile([P, P], BF16)
        masks.make_identity(nc, ident_bf16[:])
        ident_f32 = keep.tile([P, P], F32)
        masks.make_identity(nc, ident_f32[:])

        q_t = keep.tile([P, QUERY_TILES, HEADS, P], BF16)
        k_t = keep.tile([P, KV, SLOTS], BF16)
        v_codes = keep.tile([P, KV, SLOT_PASSES * HEAD_DIM], U32, align_bytes=64)
        v_scales = keep.tile([P, KV, SLOT_PASSES * HEAD_DIM], U8, align_bytes=64)
        wo_codes = keep.tile([P, FEATURE_PASSES, MODEL], U32, align_bytes=64)
        wo_scales = keep.tile([P, FEATURE_PASSES, MODEL], U8, align_bytes=64)
        a_codes = keep.tile([P, ROW_TILES, FEATURE_PASSES * P], U32, align_bytes=64)
        a_scales = keep.tile([P, ROW_TILES, FEATURE_PASSES * P], U8, align_bytes=64)

        q_rows, k_rows, v_rows, v_grouped, wo_rows, wo_grouped = {}, {}, {}, {}, {}, {}
        score_banks, bank_tops, shifts, e_rows, e_banks, e_grouped, e_mx = {}, {}, {}, {}, {}, {}, {}
        row_sums, totals, inverses, o_banks, a_rows, a_banks, a_grouped = {}, {}, {}, {}, {}, {}, {}
        panel_acc, last_acc = {}, {}

        def quantise(codes, scales, grouped):
            nc.vector.quantize_mx(out=codes.bitcast(FP8X4), scales=scales, in_=grouped)

        def transpose_blocks(bank, rows):
            for x in range(rows.shape[1] // P):
                nc.tensor.transpose(out=bank[:, x, :], in_=rows[:, x * P : (x + 1) * P], identity=ident_bf16[:])

        def transpose_words(bank, rows):
            words = rows.bitcast(F32)
            for x in range(words.shape[1] // P):
                nc.tensor.transpose(out=bank[:, x, :], in_=words[:, x * P : (x + 1) * P], identity=ident_f32[:])

        def group_words(copy, bank, grouped):
            flat = grouped.rearrange("p c r t -> p (c r t)")
            copy(
                out=flat.bitcast(F32).rearrange("p (c r u) -> p c r u", r=P, u=2),
                in_=bank[:].rearrange("p (c u) r -> p c r u", u=2),
            )
            return flat

        def warm_up():
            zeros = keep.tile([P, PANEL], BF16)
            nc.vector.memset(zeros[:], 0.0)
            bank = psum_misc.tile([P, PANEL], F32, tag="misc")
            for turn in range(6):
                nc.tensor.matmul(out=bank[:], lhsT=zeros[:, :P], rhs=zeros[:], start=True, stop=True)

        def load_queries(q_unit):
            c, query_tile = divmod(q_unit, QUERY_TILES)
            rows = loads.tile([P, TILES * HEAD_DIM], BF16, tag="q_rows")
            nc.sync.dma_start(
                out=rows[:],
                in_=q_pos[query_tile * P : (query_tile + 1) * P, c * TILES : (c + 1) * TILES, :].rearrange(
                    "q h d -> q (h d)"
                ),
            )
            q_rows[q_unit] = rows

        def transpose_queries(q_unit):
            c, query_tile = divmod(q_unit, QUERY_TILES)
            bank = psum_misc.tile([P, TILES, P], BF16, tag="misc")
            transpose_blocks(bank, q_rows[q_unit])
            nc.vector.tensor_copy(out=q_t[:, query_tile, c * TILES : (c + 1) * TILES, :], in_=bank[:])

        def load_slots(source, tag, pair):
            b, first = divmod(GROUP * pair, KV_HEADS)
            rows = loads.tile([P, SLOT_PASSES, PACK, GROUP, HEAD_DIM], BF16, tag=tag, bufs=PAIRS_AHEAD + 1)
            for c in range(SLOT_PASSES):
                nc.sync.dma_start(
                    out=rows[:, c, :, :, :].rearrange("p t g d -> p t (g d)"),
                    in_=source[b, c * K_PASS : (c + 1) * K_PASS, first : first + GROUP, :].rearrange(
                        "(p t) g d -> p t (g d)", t=PACK
                    ),
                )
            return rows

        def load_keys(pair):
            rows = load_slots(k_mem, "k_rows", pair)
            for j in range(GROUP):
                k_rows[GROUP * pair + j] = rows[:, :, :, j, :]

        def load_values(pair):
            rows = load_slots(v_mem, "v_rows", pair)
            for j in range(GROUP):
                v_rows[GROUP * pair + j] = rows[:, :, :, j, :]

        def transpose_keys(kv, copy, first=0, last=SLOT_PASSES):
            bank = psum_misc.tile([P, (last - first) * PACK, P], BF16, tag="misc")
            for x in range((last - first) * PACK):
                nc.tensor.transpose(
                    out=bank[:, x, :], in_=k_rows[kv][:, first + x // PACK, x % PACK, :], identity=ident_bf16[:]
                )
            copy(out=k_t[:, kv, first * K_PASS : last * K_PASS], in_=bank[:].rearrange("p x m -> p (x m)"))

        def group_values(kv, c):
            grouped = work.tile([P, HEAD_DIM, PACK], BF16, tag=("v_first", "v_second")[c], bufs=1, align_bytes=64)
            nc.gpsimd.tensor_scalar(
                out=grouped[:],
                in0=v_rows[kv][:, c, :, :].rearrange("p t d -> p d t"),
                scalar1=1.0,
                scalar2=0.0,
                op0=ALU.mult,
                op1=ALU.add,
            )
            v_grouped[kv, c] = grouped

        def quantise_values(kv, c):
            cols = slice(c * HEAD_DIM, (c + 1) * HEAD_DIM)
            quantise(v_codes[:, kv, cols], v_scales[:, kv, cols], v_grouped[kv, c][:].rearrange("p d t -> p (d t)"))

        def load_wo(wo_unit):
            pair, c = divmod(wo_unit, FEATURE_PASSES)
            rows = loads.tile([P, 2, K_PASS], BF16, tag="wo_rows", bufs=LOAD_AHEAD + WO_FIRST)
            nc.sync.dma_start(
                out=rows[:],
                in_=Wo[pair * WO_ROWS : (pair + 1) * WO_ROWS, c * K_PASS : (c + 1) * K_PASS].rearrange(
                    "(y p) a -> p y a", p=P
                ),
            )
            wo_rows[wo_unit] = rows

        def transpose_wo(wo_unit):
            bank = psum_misc.tile([P, 2, WO_ROWS], F32, tag="misc")
            for u in range(2):
                for y in range(2):
                    nc.tensor.transpose(
                        out=bank[:, u, y * P : (y + 1) * P],
                        in_=wo_rows[wo_unit][:, y, :].bitcast(F32)[:, u * P : (u + 1) * P],
                        identity=ident_f32[:],
                    )
            grouped = work.tile([P, WO_ROWS * PACK], BF16, tag="wo_grouped", align_bytes=64)
            nc.scalar.copy(
                out=grouped[:].bitcast(F32).rearrange("p (r u) -> p r u", u=2),
                in_=bank[:].rearrange("p u r -> p r u"),
            )
            wo_grouped[wo_unit] = grouped

        def quantise_wo(wo_unit):
            pair, c = divmod(wo_unit, FEATURE_PASSES)
            cols = slice(pair * WO_ROWS, (pair + 1) * WO_ROWS)
            quantise(wo_codes[:, c, cols], wo_scales[:, c, cols], wo_grouped[wo_unit][:])

        def place(i):
            unit, x = divmod(i, TILES)
            row_tile, c = a_order[unit]
            head = TILES * c + x
            return unit, x, head, row_tile, (row_tile // QUERY_TILES) * KV_HEADS + head // GROUP

        def scores(i):
            unit, x, head, row_tile, kv = place(i)
            score_banks[i] = []
            tops = small.tile([P, SLOT_PASSES], F32, tag="tops")
            for c in range(SLOT_PASSES):
                s = psum_scores.tile([P, K_PASS], F32, tag="s")
                if c == 0:
                    nc.tensor.matmul(
                        out=s[:, :128],
                        lhsT=q_t[:, row_tile % QUERY_TILES, head, :],
                        rhs=k_t[:, kv, :128],
                        start=True,
                        stop=True,
                    )
                nc.tensor.matmul(
                    out=s[:],
                    lhsT=q_t[:, row_tile % QUERY_TILES, head, :],
                    rhs=k_t[:, kv, c * K_PASS : (c + 1) * K_PASS],
                    start=True,
                    stop=True,
                )
                nc.vector.tensor_reduce(out=tops[:, c : c + 1], in_=s[:], axis=ALONG_ROW, op=ALU.max)
                score_banks[i].append(s)
            bank_tops[i] = tops

        def find_shift(i):
            tops = bank_tops[i]
            shift = small.tile([P, 1], F32, tag="shift")
            nc.gpsimd.tensor_scalar(
                out=shift[:], in0=tops[:, 0:1], scalar1=tops[:, 1:2], scalar2=-SCORE_FACTOR, op0=ALU.max, op1=ALU.mult
            )
            shifts[i] = shift

        def exponentials(i):
            unit, x = divmod(i, TILES)
            if x == 0:
                sums = small.tile([P, TILES, SLOT_PASSES], F32, tag="sums")
                row_sums[unit] = sums
            e = work.tile([P, SLOTS], BF16, tag="e")
            for c in range(SLOT_PASSES):
                nc.scalar.activation(
                    out=e[:, c * K_PASS : (c + 1) * K_PASS].rearrange("q (u p w) -> q u p w", u=2, w=2),
                    in_=score_banks[i][c][:].rearrange("q (u w p) -> q u p w", u=2, w=2),
                    func=EXP,
                    bias=shifts[i][:],
                    scale=SCORE_FACTOR,
                    accum_out=row_sums[unit][:, x, c : c + 1],
                )
            e_rows[i] = e

        def transpose_e(i, first=0, last=SLOT_PASSES):
            bank = psum_misc.tile([P, 2 * (last - first), P], F32, tag="misc")
            transpose_words(bank, e_rows[i][:, first * K_PASS : last * K_PASS])
            e_banks[i, first] = bank

        def group_e(i, copy, first=0, last=SLOT_PASSES):
            if first == 0:
                grouped = work.tile([P, SLOT_PASSES, P, PACK], BF16, tag="e_grouped", align_bytes=64)
                e_grouped[i] = grouped
            group_words(copy, e_banks[i, first], e_grouped[i][:, first:last, :, :])

        def quantise_e(i, first=0, last=SLOT_PASSES):
            if first == 0:
                e_codes = codes_pool.tile([P, SLOT_PASSES * P], U32, tag="e_codes", align_bytes=64)
                e_scales = codes_pool.tile([P, SLOT_PASSES * P], U8, tag="e_scales", align_bytes=64)
                e_mx[i] = (e_codes, e_scales)
            e_codes, e_scales = e_mx[i]
            cols = slice(first * P, last * P)
            quantise(e_codes[:, cols], e_scales[:, cols], e_grouped[i][:, first:last, :, :].rearrange("p c r t -> p (c r t)"))

        def add_row_sums(unit, first, last):
            total = small.tile([P, last - first], F32, tag="total")
            sums = row_sums[unit]
            nc.gpsimd.tensor_tensor(
                out=total[:], in0=sums[:, first:last, 0], in1=sums[:, first:last, 1], op=ALU.add
            )
            totals[unit, first] = total

        def invert_row_sums(unit, first, last):
            inverse = small.tile([P, last - first], F32, tag="inverse")
            nc.vector.reciprocal(out=inverse[:], in_=totals[unit, first][:])
            inverses[unit, first] = inverse

        def weigh_values(unit, first, last):
            if first == 0:
                a = work.tile([P, TILES, HEAD_DIM], BF16, tag="a")
                a_rows[unit] = a
            o = psum_misc.tile([P, last - first, HEAD_DIM], F32, tag="misc")
            for x in range(first, last):
                kv = place(unit * TILES + x)[4]
                e_codes, e_scales = e_mx[unit * TILES + x]
                for c in range(SLOT_PASSES):
                    cols = slice(c * P, (c + 1) * P)
                    nc.tensor.matmul_mx(
                        out=o[:, x - first, :],
                        lhsT=e_codes[:, cols].bitcast(FP8X4),
                        lhsT_scale=e_scales[:, cols],
                        rhs=v_codes[:, kv, cols].bitcast(FP8X4),
                        rhs_scale=v_scales[:, kv, cols],
                        start=(c == 0),
                        stop=(c == SLOT_PASSES - 1),
                    )
            o_banks[unit, first] = o

        def divide(unit, first, last):
            nc.vector.tensor_tensor(
                out=a_rows[unit][:, first:last, :],
                in0=o_banks[unit, first][:],
                in1=inverses[unit, first][:].unsqueeze(2).broadcast_to([P, last - first, HEAD_DIM]),
                op=ALU.mult,
            )

        def transpose_a(unit, first, last):
            if first == 0:
                bank = psum_misc.tile([P, 2, P], F32, tag="misc")
                a_banks[unit] = bank
            words = a_rows[unit][:].rearrange("q x d -> q (x d)").bitcast(F32)
            for u in range(2):
                if first < 2 * (u + 1) <= last:
                    nc.tensor.transpose(
                        out=a_banks[unit][:, u, :], in_=words[:, u * P : (u + 1) * P], identity=ident_f32[:]
                    )
            if last == TILES:
                grouped = work.tile([P, 1, P, PACK], BF16, tag="a_grouped", align_bytes=64)
                a_grouped[unit] = group_words(nc.scalar.copy, a_banks[unit], grouped[:])

        def quantise_a(unit):
            row_tile, c = a_order[unit]
            cols = slice(c * P, (c + 1) * P)
            quantise(a_codes[:, row_tile, cols], a_scales[:, row_tile, cols], a_grouped[unit])

        def project_passes(acc, row_tile, n, passes):
            cols = slice(n * PANEL, (n + 1) * PANEL)
            for c in passes:
                nc.tensor.matmul_mx(
                    out=acc[:],
                    lhsT=a_codes[:, row_tile, c * P : (c + 1) * P].bitcast(FP8X4),
                    lhsT_scale=a_scales[:, row_tile, c * P : (c + 1) * P],
                    rhs=wo_codes[:, c, cols].bitcast(FP8X4),
                    rhs_scale=wo_scales[:, c, cols],
                    start=(c == 0),
                    stop=(c == FEATURE_PASSES - 1),
                )

        def store_panel(acc, row_tile, n, copy):
            b, query_tile = divmod(row_tile, QUERY_TILES)
            result = work.tile([P, PANEL], F32, tag="result", bufs=PANELS)
            copy(out=result[:], in_=acc[:])
            nc.sync.dma_start(
                out=out[b, query_tile * P : (query_tile + 1) * P, n * PANEL : (n + 1) * PANEL], in_=result[:]
            )

        def start_last_panels(n):
            acc = psum_scores.tile([P, PANEL], F32, tag="s")
            project_passes(acc, last_row_tile, n, range(FEATURE_PASSES - 2))
            last_acc[n] = acc

        def project(row_tile, n, half, copy):
            if half == 0:
                acc = psum_misc.tile([P, PANEL], F32, tag="misc")
                panel_acc[row_tile, n] = acc
            acc = panel_acc[row_tile, n]
            project_passes(acc, row_tile, n, range(half * FEATURE_PASSES // 2, (half + 1) * FEATURE_PASSES // 2))
            if half == 1:
                store_panel(acc, row_tile, n, copy)

        load_queries(0)
        load_keys(0)
        for wo_unit in range(WO_FIRST):
            load_wo(wo_unit)
        load_values(0)
        for n in range(1, LOAD_AHEAD + 1):
            load_queries(n)
            load_wo(WO_FIRST + n - 1)
            if n <= PAIRS_AHEAD:
                load_keys(n)
                load_values(n)
        warm_up()
        transpose_keys(0, nc.scalar.copy, 0, 1)
        transpose_queries(0)
        transpose_keys(0, nc.scalar.copy, 1, 2)
        transpose_wo(0)

        panels = [(row_tile, n) for n in range(PANELS) for row_tile in range(QUERY_TILES)]
        panels += [(row_tile, n) for row_tile in range(QUERY_TILES, ROW_TILES - 1) for n in range(PANELS)]
        last_row_tile = ROW_TILES - 1
        for tick in range(HEAD_TILES):
            kv, c = divmod(tick - VALUES_START, PREP_PERIOD)
            if c < SLOT_PASSES and 0 <= kv < KV:
                quantise_values(kv, c)
                if kv + 1 < KV:
                    group_values(kv + 1, c)
                pair = (kv + 1) // GROUP + PAIRS_AHEAD + 1
                if c == SLOT_PASSES - 1 and (kv + 1) % GROUP == GROUP - 1 and pair < KV // GROUP:
                    load_values(pair)

            scores(tick)
            find_shift(tick)

            unit, rest = divmod(tick - (TILES - 1) - DIVIDE_LAG, TILES)
            if rest == 0 and 0 <= unit:
                divide(unit, 0, TILES)

            if tick < SLOT_PASSES:
                group_values(0, tick)

            if tick >= EXP_LAG:
                exponentials(tick - EXP_LAG)

            if tick >= TRANSPOSE_LAG:
                transpose_e(tick - TRANSPOSE_LAG)
                group_e(tick - TRANSPOSE_LAG, nc.scalar.copy)

            if tick >= QUANTISE_LAG:
                quantise_e(tick - QUANTISE_LAG)

            unit, rest = divmod(tick - (TILES - 1) - SUM_LAG, TILES)
            if rest == 0 and 0 <= unit:
                add_row_sums(unit, 0, TILES)

            unit, rest = divmod(tick - (TILES - 1) - INVERT_LAG, TILES)
            if rest == 0 and 0 <= unit:
                invert_row_sums(unit, 0, TILES)

            unit, rest = divmod(tick - (TILES - 1) - A_LAG, TILES)
            if rest == 0 and 0 <= unit:
                transpose_a(unit, 0, TILES)

            if tick == 0:
                for wo_unit in range(1, WO_FIRST):
                    transpose_wo(wo_unit)
            round_, rest = divmod(tick - WO_START, PREP_PERIOD)
            wo_unit = WO_FIRST + 2 * round_ + rest
            if rest < 2 and WO_FIRST <= wo_unit < WO_UNITS:
                transpose_wo(wo_unit)
                if wo_unit + LOAD_AHEAD < WO_UNITS:
                    load_wo(wo_unit + LOAD_AHEAD)

            kv, rest = divmod(tick, PREP_PERIOD)
            kv += 1
            if (rest == 1 or tick == 0) and tick != 1 and kv < KV:
                transpose_keys(kv, nc.vector.tensor_copy)
                pair = kv // GROUP + PAIRS_AHEAD + 1
                if kv % GROUP == GROUP - 1 and pair < KV // GROUP:
                    load_keys(pair)

            panel, half = divmod(tick - PROJECT_START, 2)
            if 0 <= panel < len(panels):
                project(*panels[panel], half, nc.vector.tensor_copy if panel % 2 == 0 else nc.scalar.copy)

            unit, rest = divmod(tick - (TILES - 1) - VALUES_LAG, TILES)
            if rest == 0 and 0 <= unit:
                weigh_values(unit, 0, TILES)

            q_unit, rest = divmod(tick, PREP_PERIOD)
            q_unit += 1
            if rest == 2 and q_unit < Q_UNITS:
                transpose_queries(q_unit)
                if q_unit + LOAD_AHEAD < Q_UNITS:
                    load_queries(q_unit + LOAD_AHEAD)

            unit, rest = divmod(tick - (TILES - 1) - A_LAG, TILES)
            if rest == 1 and 0 <= unit:
                quantise_a(unit)

            if 1 <= tick <= WO_FIRST:
                quantise_wo(tick - 1)
            round_, rest = divmod(tick - WO_START, PREP_PERIOD)
            wo_unit = WO_FIRST + 2 * round_ + rest
            if rest < 2 and WO_FIRST < wo_unit <= WO_UNITS:
                quantise_wo(wo_unit - 1)

        unit, x, i = A_UNITS - 1, TILES - 1, HEAD_TILES - 1
        divide(unit - 1, 0, TILES)
        quantise_e(i - 2)
        exponentials(i)
        transpose_e(i - 1)
        group_e(i - 1, nc.vector.tensor_copy)
        start_last_panels(0)
        transpose_a(unit - 1, 0, TILES)
        start_last_panels(1)
        quantise_e(i - 1)
        transpose_e(i, 0, 1)
        group_e(i, nc.vector.tensor_copy, 0, 1)
        transpose_e(i, 1, 2)
        group_e(i, nc.scalar.copy, 1, 2)
        add_row_sums(unit, 0, x)
        quantise_e(i, 0, 1)
        weigh_values(unit, 0, x)
        start_last_panels(2)
        add_row_sums(unit, x, TILES)
        quantise_e(i, 1, 2)
        weigh_values(unit, x, TILES)
        invert_row_sums(unit, 0, x)
        quantise_a(unit - 1)
        divide(unit, 0, x)
        invert_row_sums(unit, x, TILES)
        start_last_panels(3)
        transpose_a(unit, 0, x)
        divide(unit, x, TILES)
        transpose_a(unit, x, TILES)
        for n in range(PANELS):
            project_passes(last_acc[n], last_row_tile, n, range(FEATURE_PASSES - 2, FEATURE_PASSES - 1))
        quantise_a(unit)
        for n in range(PANELS):
            project_passes(last_acc[n], last_row_tile, n, range(FEATURE_PASSES - 1, FEATURE_PASSES))
            store_panel(last_acc[n], last_row_tile, n, nc.vector.tensor_copy if n % 2 == 0 else nc.scalar.copy)
